import numpy as np
import ml_dtypes


def mxq(x, axis, fmt="e4m3"):
    dtype, down = {"e4m3": (ml_dtypes.float8_e4m3fn, 7), "e5m2": (ml_dtypes.float8_e5m2, 14)}[fmt]
    v = np.moveaxis(np.asarray(x, np.float32).astype(ml_dtypes.bfloat16).astype(np.float64), axis, -1)
    blocks = v.reshape(v.shape[:-1] + (-1, 32))
    amax = np.abs(blocks).max(-1, keepdims=True)
    byte = np.maximum(np.where(amax > 0, np.frexp(amax)[1] - 1 + 127, 0) - down, 1)
    scale = np.exp2(byte - 127.0)
    codes = (blocks / scale).astype(np.float32).astype(dtype).astype(np.float64)
    return np.moveaxis((codes * scale).reshape(v.shape), -1, axis)


WIDE = False


def mx_kscale(k):
    if not WIDE:
        return np.ones(k)
    levels = np.array([10, -10, 5, -5, 0])
    a = np.random.permutation(np.resize(levels, k // 512 * 4)).reshape(k // 512, 4)
    idx = np.arange(k)
    return np.exp2(a[idx // 512, idx % 128 // 32])


BF16 = ml_dtypes.bfloat16


def bf(x):
    return np.asarray(x, np.float32).astype(BF16)


def f64(x):
    return np.asarray(x).astype(np.float64)


B, IN, H, G, GA, GB = 4096, 512, 512, 6, 4, 2
EPS = 1e-5


def layer_norm(v, g, b):
    mu = v.mean(-1, keepdims=True)
    var = np.square(v - mu).mean(-1, keepdims=True)
    return (v - mu) / np.sqrt(var + EPS) * g + b


def sigmoid(v):
    return 1.0 / (1.0 + np.exp(-v))


def setup_inputs():
    s, t = mx_kscale(IN), mx_kscale(H)
    return {"x": bf(np.random.standard_normal((B, IN)) * s),
            "h": bf(np.random.standard_normal((B, H)) * t),
            "W_r": bf(np.random.standard_normal((H, H)) / np.sqrt(H) / t),
            "U_r": bf(np.random.standard_normal((H, IN)) / np.sqrt(IN) / s),
            "W_c": bf(np.random.standard_normal((H, H)) / np.sqrt(H) / t),
            "U_c": bf(np.random.standard_normal((H, IN)) / np.sqrt(IN) / s),
            "ln_gamma": bf(1.0 + 0.1 * np.random.standard_normal((GA, H))),
            "ln_beta": bf(0.2 * np.random.standard_normal((GA, H)))}


def reference(x, h, W_r, U_r, W_c, U_c, ln_gamma, ln_beta):
    g_rh, g_rx, g_ch, g_cx = f64(ln_gamma)
    b_rh, b_rx, b_ch, b_cx = f64(ln_beta)
    hf = f64(h)
    xq = mxq(f64(x), 1, "e4m3")
    r = sigmoid(layer_norm(mxq(hf, 1, "e4m3") @ mxq(f64(W_r), 1, "e4m3").T, g_rh, b_rh)
                + layer_norm(xq @ mxq(f64(U_r), 1, "e4m3").T, g_rx, b_rx))
    return np.tanh(layer_norm(mxq(hf * r, 1, "e4m3") @ mxq(f64(W_c), 1, "e4m3").T, g_ch, b_ch)
                   + layer_norm(xq @ mxq(f64(U_c), 1, "e4m3").T, g_cx, b_cx))

@@ -1,0 +1,424 @@
+from contextlib import ExitStack
+
+import concourse.mybir as mybir
+from concourse.masks import make_identity
+
+F32 = mybir.dt.float32
+BF16 = mybir.dt.bfloat16
+U32 = mybir.dt.uint32
+U8 = mybir.dt.uint8
+FP8X4 = mybir.dt.float8_e4m3fn_x4
+ACT = mybir.ActivationFunctionType
+ALU = mybir.AluOpType
+
+P = 128
+ROWS = 4096
+D = 512
+ST = 512
+NST = ROWS // ST
+NJ = ST // P
+NT = D // P
+EPS = 1e-5
+FLOPS = 4 * 2 * ROWS * D * D
+
+MANUAL = True
+UNITS = [(0, 1), (1, 1), (2, 1), (3, 1), (0, 2), (4, 1), (1, 2), (5, 1), (2, 2), (6, 1), (3, 2), (7, 1),
+         (4, 2), (5, 2), (6, 2), (7, 2)]
+LA = 1
+LBP = 4
+LCP = 8
+LD = 13
+LPREP = [0, 5, 5, 5, 8, 8, 8, 8]
+LLOAD = 14
+V_BUFS = 5
+TA_BUFS = 1
+PE_ORDER = ["ta", "mx", "tb", "tz"]
+G_ROWS = 64
+FIX_V = 18
+FIX_S = 60
+BIAS = 0
+FORCE_A = 62
+FORCE_B = 60
+
+
+def tile_layernormgrucell_pa_t_kernel(tc, x, h, W_r, U_r, W_c, U_c, ln_gamma, ln_beta, out):
+    nc = tc.nc
+    x_v = x.rearrange("(s j p) k -> p s j k", s=NST, j=NJ)
+    h_v = h.rearrange("(s j p) k -> p s j k", s=NST, j=NJ)
+    out_v = out.rearrange("(s j p) f -> p s j f", s=NST, j=NJ)
+
+    with ExitStack() as ctx:
+        if MANUAL:
+            ctx.enter_context(tc.manual_schedule())
+        const = ctx.enter_context(tc.tile_pool(name="const", bufs=1))
+        wp = ctx.enter_context(tc.tile_pool(name="wp", bufs=2))
+        io = ctx.enter_context(tc.tile_pool(name="io", bufs=3))
+        grp = ctx.enter_context(tc.tile_pool(name="grp", bufs=2))
+        qp = ctx.enter_context(tc.tile_pool(name="qp", bufs=3))
+        npool = ctx.enter_context(tc.tile_pool(name="npool", bufs=3))
+        zpool = ctx.enter_context(tc.tile_pool(name="zpool", bufs=4))
+        opool = ctx.enter_context(tc.tile_pool(name="opool", bufs=4))
+        sm = ctx.enter_context(tc.tile_pool(name="sm", bufs=6))
+        psV = ctx.enter_context(tc.psum_pool(name="psV", bufs=V_BUFS))
+        psT = ctx.enter_context(tc.psum_pool(name="psT", bufs=1))
+
+        work = {"v": 0, "s": 0}
+
+        def did(eng, cols):
+            work[eng] += cols + (FIX_V if eng == "v" else FIX_S)
+
+        def pick(cols, force=False):
+            eng = "v" if force or work["v"] + FIX_V + BIAS < work["s"] + FIX_S else "s"
+            did(eng, cols)
+            return eng
+
+        def evac(dst, src, cols):
+            if pick(cols) == "v":
+                nc.vector.tensor_copy(out=dst, in_=src)
+            else:
+                nc.scalar.copy(out=dst, in_=src)
+
+        def affine(dst, src, mul, add, sub_first, force):
+            if pick(D, force) == "v":
+                if sub_first is None:
+                    nc.vector.tensor_scalar(out=dst, in0=src, scalar1=mul, scalar2=add, op0=ALU.mult, op1=ALU.add)
+                else:
+                    nc.vector.tensor_scalar(out=dst, in0=src, scalar1=sub_first, scalar2=mul, op0=ALU.subtract, op1=ALU.mult)
+            else:
+                nc.scalar.activation(out=dst, in_=src, func=ACT.Identity, bias=add, scale=mul)
+
+        def quant(codes, scales, src, cols):
+            nc.vector.quantize_mx(out=codes.bitcast(FP8X4), scales=scales, in_=src)
+            did("v", cols // 4)
+
+        ident = const.tile([P, P], F32, name="ident")
+        make_identity(nc, ident[:])
+        mhalf = const.tile([P, 2], F32, name="mhalf")
+        nc.gpsimd.memset(mhalf[:], -0.5)
+        warm = const.tile([P, 1], F32, name="warm")
+        nc.vector.memset(warm[:], 0.0)
+        nc.scalar.activation(out=warm[:], in_=warm[:], func=ACT.Sigmoid)
+
+        xh = {}
+
+        def load(s):
+            h_sb = io.tile([P, NJ, D], BF16, tag="h_sb")
+            nc.sync.dma_start(out=h_sb[:], in_=h_v[:, s])
+            x_sb = io.tile([P, NJ, D], BF16, tag="x_sb")
+            nc.sync.dma_start(out=x_sb[:], in_=x_v[:, s])
+            xh[s] = (h_sb, x_sb)
+
+        wraw = {}
+
+        def load_weight(i, w_ap, permuted):
+            raw = wp.tile([P, NT, D], BF16, tag="wraw", bufs=4)
+            if permuted:
+                nc.sync.dma_start(
+                    out=raw[:].rearrange("p (u e) k -> p u e k", u=2),
+                    in_=w_ap.rearrange("(u p e) k -> p u e k", u=2, e=2),
+                )
+            else:
+                nc.sync.dma_start(out=raw[:], in_=w_ap.rearrange("(t p) k -> p t k", p=P))
+            wraw[i] = raw
+
+        wq = [const.tile([P, D], U32, name="wq%d" % i, align_bytes=64) for i in range(4)]
+        ws = [const.tile([P, D], U8, name="ws%d" % i, align_bytes=64) for i in range(4)]
+        wg = {}
+
+        def words_to_bank(pool, tag, src, first):
+            tp = pool.tile([P, 2, 256], F32, tag=tag)
+            for oo in range(2):
+                w32 = src[:, first + oo, :].bitcast(F32)
+                for u in range(2):
+                    nc.tensor.transpose(tp[:, u, oo * P:(oo + 1) * P], w32[:, u * P:(u + 1) * P], ident[:])
+            return tp
+
+        def bank_to_group(dst, half, tp):
+            d32 = dst[:].bitcast(F32).rearrange("p (n u) -> p n u", u=2)
+            evac(d32[:, half * 256:(half + 1) * 256, :], tp[:].rearrange("p u n -> p n u"), D)
+
+        def w_pe_ev(i, b, pool, tag):
+            if b == 0:
+                gw = wp.tile([P, 4 * D], BF16, tag="gw", align_bytes=64)
+                wg[i] = gw
+            bank_to_group(wg[i], b, words_to_bank(pool, tag, wraw[i], 2 * b))
+
+        def w_q(i):
+            quant(wq[i][:], ws[i][:], wg[i][:], 4 * D)
+
+        xq = const.tile([P, NST, ST], U32, name="xq", align_bytes=64)
+        xs = const.tile([P, NST, ST], U8, name="xs", align_bytes=64)
+        hq = {}
+        gh = {}
+        gx = {}
+        ptp = {}
+
+        def p_pe(s, k, pool=None, tag="tz"):
+            if k == 0:
+                g_h = grp.tile([P, 4 * ST], BF16, tag="gh", bufs=5, align_bytes=64)
+                g_x = grp.tile([P, 4 * ST], BF16, tag="gx", align_bytes=64)
+                gh[s] = g_h
+                gx[s] = g_x
+            ptp[(s, k)] = words_to_bank(pool or psT, tag, xh[s][k // 2], 2 * (k % 2))
+
+        def p_ev(s, k):
+            bank_to_group(gh[s] if k < 2 else gx[s], k % 2, ptp[(s, k)])
+
+        def p_q(s, which):
+            if which == 0:
+                hq_c = qp.tile([P, ST], U32, tag="hq", align_bytes=64)
+                hq_s = qp.tile([P, ST], U8, tag="hs", align_bytes=64)
+                quant(hq_c[:], hq_s[:], gh[s][:], 4 * ST)
+                hq[s] = (hq_c, hq_s)
+            else:
+                quant(xq[:, s, :], xs[:, s, :], gx[s][:], 4 * ST)
+
+        def prep_params():
+            pr_str = pr32[:].rearrange("p (u q e) -> p u e q", u=2, e=2)
+            res = []
+            for kind in range(2):
+                tp = psT.tile([P, NT, P], F32, tag="tb")
+                for t in range(NT):
+                    src = pr_str[:, t // 2, t % 2, :] if kind == 0 else pr32[:, t * P:(t + 1) * P]
+                    nc.tensor.transpose(tp[:, t, :], src, ident[:])
+                tab = const.tile([P, 8, NT], F32, name="prm%d" % kind)
+                nc.vector.tensor_copy(out=tab[:], in_=tp[:, :, 0:8].rearrange("p c i -> p i c"))
+                bs = const.tile([P, NT], F32, name="bs%d" % kind)
+                nc.vector.tensor_tensor(out=bs[:], in0=tab[:, 4 + 2 * kind, :], in1=tab[:, 5 + 2 * kind, :], op=ALU.add)
+                res.append((tab, bs))
+            return res
+
+        nab = {}
+        ztl = {}
+        hrq = {}
+        vab = {}
+        sca = {}
+
+        def a_pe(unit, j):
+            s, stage = unit
+            js = slice(j * P, (j + 1) * P)
+            a_c, a_s_ = hq[s] if stage == 1 else hrq[s]
+            wa, wb = (0, 1) if stage == 1 else (2, 3)
+            va = psV.tile([P, D], F32, tag="v")
+            nc.tensor.matmul_mx(out=va[:], lhsT=a_c[:, js].bitcast(FP8X4), lhsT_scale=a_s_[:, js],
+                                rhs=wq[wa][:].bitcast(FP8X4), rhs_scale=ws[wa][:], start=True, stop=True)
+            vb = psV.tile([P, D], F32, tag="v")
+            nc.tensor.matmul_mx(out=vb[:], lhsT=xq[:, s, js].bitcast(FP8X4), lhsT_scale=xs[:, s, js],
+                                rhs=wq[wb][:].bitcast(FP8X4), rhs_scale=ws[wb][:], start=True, stop=True)
+            vab[(unit, j)] = (va, vb)
+
+        def a_v(unit, j):
+            va, vb = vab[(unit, j)]
+            st = sm.tile([P, 2, 6], F32, tag="st")
+            nc.vector.bn_stats(out=st[:, 0, :], in_=va[:])
+            nc.vector.bn_stats(out=st[:, 1, :], in_=vb[:])
+            mv = sm.tile([P, 2, 2], F32, tag="mv")
+            nc.vector.bn_aggr(out=mv[:, 0, :], in_=st[:, 0, :])
+            nc.vector.bn_aggr(out=mv[:, 1, :], in_=st[:, 1, :])
+            did("v", D)
+            did("v", D)
+            did("v", 54)
+            did("v", 54)
+            ve = sm.tile([P, 2], F32, tag="ve")
+            nc.gpsimd.tensor_scalar(out=ve[:], in0=mv[:, :, 1], scalar1=1.0, scalar2=EPS, op0=ALU.mult, op1=ALU.add)
+            rs = sm.tile([P, 2], F32, tag="rs")
+            nc.gpsimd.tensor_tensor(out=rs[:], in0=ve[:], in1=mhalf[:], op=ALU.pow)
+            mr = sm.tile([P, 2], F32, tag="mr")
+            nc.gpsimd.tensor_tensor(out=mr[:], in0=mv[:, :, 0], in1=rs[:], op=ALU.mult)
+            cc = sm.tile([P, 2], F32, tag="cc")
+            nc.gpsimd.tensor_scalar(out=cc[:], in0=mr[:], scalar1=-1.0, scalar2=0.0, op0=ALU.mult, op1=ALU.add)
+            sca[(unit, j)] = (rs, cc, mv)
+
+        def a_s(unit, j):
+            if j == 0:
+                na = npool.tile([P, NJ, D], F32, tag="na")
+                nb = npool.tile([P, NJ, D], F32, tag="nb")
+                nab[unit] = (na, nb)
+            rs, cc, mv = sca[(unit, j)]
+            for w in range(2):
+                affine(nab[unit][w][:, j, :], vab[(unit, j)][w][:], rs[:, w:w + 1], cc[:, w:w + 1], mv[:, w, 0:1],
+                       4 * UNITS.index(unit) + j >= FORCE_A)
+
+        tab_ = {}
+
+        def b_pe(unit, t, which):
+            src = nab[unit][which]
+            if UNITS.index(unit) == len(UNITS) - 1 and t % 2 == 1:
+                tt = psV.tile([P, ST], F32, tag="v")
+            else:
+                tt = psT.tile([P, ST], F32, tag="ta" if which == 0 else "tb", bufs=TA_BUFS if which == 0 else 1)
+            for j in range(NJ):
+                nc.tensor.transpose(tt[:, j * P:(j + 1) * P], src[:, j, t * P:(t + 1) * P], ident[:])
+            tab_[(unit, t, which)] = tt
+
+        def b_s(unit, t):
+            stage = unit[1]
+            if t == 0:
+                zt = zpool.tile([P, NT, ST], F32, tag="zt")
+                ztl[unit] = zt
+            tab, bs = tabs[stage - 1]
+            affine(ztl[unit][:, t, :], tab_[(unit, t, 0)][:], tab[:, 2 * stage - 2, t:t + 1], bs[:, t:t + 1], None,
+                   4 * UNITS.index(unit) + t >= FORCE_B)
+
+        def b_v(unit, t):
+            stage = unit[1]
+            tab, bs = tabs[stage - 1]
+            zt = ztl[unit]
+            nc.vector.scalar_tensor_tensor(out=zt[:, t, :], in0=tab_[(unit, t, 1)][:], scalar=tab[:, 2 * stage - 1, t:t + 1],
+                                           in1=zt[:, t, :], op0=ALU.mult, op1=ALU.add)
+            did("v", ST)
+
+        zol = {}
+
+        def c_pe(unit, i):
+            if unit[1] == 1:
+                return
+            zt = ztl[unit]
+            if UNITS.index(unit) >= len(UNITS) - 2 and i % 2 == 1:
+                zo = psV.tile([P, D], F32, tag="v")
+            elif UNITS.index(unit) == len(UNITS) - 1 and i == 2:
+                zo = psT.tile([P, D], F32, tag="ta")
+            else:
+                zo = psT.tile([P, D], F32, tag="tz")
+            for t in range(NT):
+                nc.tensor.transpose(zo[:, t * P:(t + 1) * P], zt[:, t, i * P:(i + 1) * P], ident[:])
+            zol[(unit, i)] = zo
+
+        def c_s(unit, i):
+            s, stage = unit
+            zt = ztl[unit]
+            did("s", D)
+            if stage == 1:
+                nc.scalar.activation(out=zt[:, i, :], in_=zt[:, i, :], func=ACT.Sigmoid)
+            else:
+                o_sb = opool.tile([P, D], F32, tag="o")
+                nc.scalar.activation(out=o_sb[:], in_=zol[(unit, i)][:], func=ACT.Tanh)
+                nc.sync.dma_start(out=out_v[:, s, i, :], in_=o_sb[:])
+
+        ghr = {}
+
+        def d_v(unit, i):
+            s, stage = unit
+            if stage != 1:
+                return
+            zt = ztl[unit]
+            if i == 0:
+                g_hr = grp.tile([P, 4 * ST], BF16, tag="ghr", align_bytes=64)
+                ghr[s] = g_hr
+            for eng, lo, hi in ((nc.gpsimd, 0, G_ROWS), (nc.vector, G_ROWS, P)):
+                if hi > lo:
+                    rr = slice(i * P + lo, i * P + hi)
+                    eng.tensor_tensor(
+                        out=ghr[s][:].rearrange("p (r t) -> p r t", t=4)[:, rr, :],
+                        in0=zt[:, :, rr].rearrange("p t r -> p r t"),
+                        in1=gh[s][:].rearrange("p (r t) -> p r t", t=4)[:, rr, :],
+                        op=ALU.mult,
+                    )
+            if G_ROWS < P:
+                did("v", 4 * (P - G_ROWS))
+
+        def d_q(unit, i):
+            s, stage = unit
+            if stage != 1:
+                return
+            if i == 0:
+                c_c = qp.tile([P, ST], U32, tag="hrq", bufs=4, align_bytes=64)
+                c_s_ = qp.tile([P, ST], U8, tag="hrs", bufs=4, align_bytes=64)
+                hrq[s] = (c_c, c_s_)
+            c_c, c_s_ = hrq[s]
+            rr = slice(i * P, (i + 1) * P)
+            quant(c_c[:, rr], c_s_[:, rr], ghr[s][:, i * 4 * P:(i + 1) * 4 * P], 4 * P)
+
+        load_weight(0, W_r, True)
+        load(0)
+        load_weight(1, U_r, True)
+        pr_bf = const.tile([P, D], BF16, name="pr_bf")
+        nc.vector.memset(pr_bf[:], 0.0)
+        nc.sync.dma_start(out=pr_bf[0:4, :], in_=ln_gamma)
+        nc.sync.dma_start(out=pr_bf[4:8, :], in_=ln_beta)
+        load(1)
+        load_weight(2, W_c, False)
+        load_weight(3, U_c, False)
+        load(2)
+
+        n = len(UNITS)
+        nslot = 4 * n
+        first1 = {}
+        for u in range(n):
+            if UNITS[u][1] == 1:
+                first1[UNITS[u][0]] = 4 * u
+
+        def task(k):
+            return (UNITS[k // 4], k % 4) if 0 <= k < nslot else None
+
+        def run(fn, k):
+            tk = task(k)
+            if tk is not None:
+                fn(tk[0], tk[1])
+
+        w_pe_ev(0, 0, psV, "v")
+        w_pe_ev(0, 1, psV, "v")
+        p_pe(0, 0, psV, "v")
+        p_ev(0, 0)
+        p_pe(0, 1, psV, "v")
+        p_ev(0, 1)
+        w_q(0)
+        p_pe(0, 2, psT, "tb")
+        p_ev(0, 2)
+        p_pe(0, 3, psT, "tz")
+        p_ev(0, 3)
+        p_q(0, 0)
+        w_pe_ev(1, 0, psT, "ta")
+        w_pe_ev(1, 1, psV, "v")
+        p_q(0, 1)
+        w_q(1)
+        pr32 = const.tile([P, D], F32, name="pr32")
+        nc.gpsimd.tensor_scalar(out=pr32[:], in0=pr_bf[:], scalar1=1.0, scalar2=0.0, op0=ALU.mult, op1=ALU.add)
+        run(a_pe, 0)
+
+        tabs = []
+        for it in range(-1, nslot + LD + 2):
+            run(b_s, it - LBP - 1)
+            run(a_v, it)
+            run(a_s, it - LA)
+            run(b_v, it - LBP - 1)
+            run(c_s, it - LCP - 1)
+            run(d_v, it - LD)
+            run(d_q, it - LD - 1)
+            for s in range(1, NST):
+                k = it - (first1[s] - LPREP[s]) - 1
+                tight = LPREP[s] < 6
+                if 0 <= k < 4:
+                    p_ev(s, k)
+                if k == (2 if tight else 3):
+                    p_q(s, 0)
+                if k == (3 if tight else 4):
+                    p_q(s, 1)
+            if it == 2:
+                w_q(2)
+            if it == 4:
+                w_q(3)
+            for what in PE_ORDER:
+                if what == "ta":
+                    tk = task(it - LBP)
+                    if tk is not None:
+                        b_pe(tk[0], tk[1], 0)
+                    if 0 <= it < 4:
+                        w_pe_ev(2 + it // 2, it % 2, psT, "ta")
+                if what == "tb":
+                    tk = task(it - LBP)
+                    if tk is not None:
+                        b_pe(tk[0], tk[1], 1)
+                    if it == 1:
+                        tabs.extend(prep_params())
+                if what == "mx" and it >= 0:
+                    run(a_pe, it + 1)
+                if what == "tz":
+                    run(c_pe, it - LCP)
+                    for s in range(1, NST):
+                        k = it - (first1[s] - LPREP[s])
+                        if 0 <= k < 4:
+                            p_pe(s, k)
+            for s in range(3, NST):
+                if it == max(first1[s] - LLOAD, -1 + 2 * (s - 3)):
+                    load(s)

@@ -37,6 +37,7 @@ G_ROWS = 64
 FIX_V = 18
 FIX_S = 60
 BIAS = 0
+MX_REP = 2
 FORCE_A = 62
 FORCE_B = 60
 
@@ -200,11 +201,12 @@ def tile_layernormgrucell_pa_t_kernel(tc, x, h, W_r, U_r, W_c, U_c, ln_gamma, ln
             a_c, a_s_ = hq[s] if stage == 1 else hrq[s]
             wa, wb = (0, 1) if stage == 1 else (2, 3)
             va = psV.tile([P, D], F32, tag="v")
-            nc.tensor.matmul_mx(out=va[:], lhsT=a_c[:, js].bitcast(FP8X4), lhsT_scale=a_s_[:, js],
-                                rhs=wq[wa][:].bitcast(FP8X4), rhs_scale=ws[wa][:], start=True, stop=True)
             vb = psV.tile([P, D], F32, tag="v")
-            nc.tensor.matmul_mx(out=vb[:], lhsT=xq[:, s, js].bitcast(FP8X4), lhsT_scale=xs[:, s, js],
-                                rhs=wq[wb][:].bitcast(FP8X4), rhs_scale=ws[wb][:], start=True, stop=True)
+            for rep in range(MX_REP):
+                nc.tensor.matmul_mx(out=va[:], lhsT=a_c[:, js].bitcast(FP8X4), lhsT_scale=a_s_[:, js],
+                                    rhs=wq[wa][:].bitcast(FP8X4), rhs_scale=ws[wa][:], start=True, stop=True)
+                nc.tensor.matmul_mx(out=vb[:], lhsT=xq[:, s, js].bitcast(FP8X4), lhsT_scale=xs[:, s, js],
+                                    rhs=wq[wb][:].bitcast(FP8X4), rhs_scale=ws[wb][:], start=True, stop=True)
             vab[(unit, j)] = (va, vb)
 
         def a_v(unit, j):

@@ -22,22 +22,25 @@ EPS = 1e-5
 FLOPS = 4 * 2 * ROWS * D * D
 
 MANUAL = True
-UNITS = [(0, 1), (1, 1), (2, 1), (3, 1), (0, 2), (4, 1), (1, 2), (5, 1), (2, 2), (6, 1), (3, 2), (7, 1),
+UNITS = [(0, 1), (1, 1), (2, 1), (3, 1), (4, 1), (0, 2), (5, 1), (1, 2), (6, 1), (2, 2), (7, 1), (3, 2),
          (4, 2), (5, 2), (6, 2), (7, 2)]
-LA = 1
-LBP = 4
-LCP = 8
-LD = 13
-LPREP = [0, 5, 5, 5, 8, 8, 8, 8]
-LLOAD = 14
-V_BUFS = 5
-TA_BUFS = 1
-PE_ORDER = ["ta", "mx", "tb", "tz"]
+GB = 2
+LN = 4
+LB = LN + 5
+LC = LB + 4
+LD = LC + 4
+LPREP = [0, 5, 5, 5, 5, 8, 8, 8]
+DQ = 2
+S_EVAC = [3]
+LLOAD = 3
+V_BUFS = 4
+T_BUFS = 4
+PE_ORDER = ["ta", "tb", "tz", "mx"]
 G_ROWS = 64
 FIX_V = 18
 FIX_S = 60
 BIAS = 0
-MX_REP = 2
+EVAC_V = True
 FORCE_A = 62
 FORCE_B = 60
 
@@ -53,7 +56,7 @@ def tile_layernormgrucell_pa_t_kernel(tc, x, h, W_r, U_r, W_c, U_c, ln_gamma, ln
             ctx.enter_context(tc.manual_schedule())
         const = ctx.enter_context(tc.tile_pool(name="const", bufs=1))
         wp = ctx.enter_context(tc.tile_pool(name="wp", bufs=2))
-        io = ctx.enter_context(tc.tile_pool(name="io", bufs=3))
+        io = ctx.enter_context(tc.tile_pool(name="io", bufs=2))
         grp = ctx.enter_context(tc.tile_pool(name="grp", bufs=2))
         qp = ctx.enter_context(tc.tile_pool(name="qp", bufs=3))
         npool = ctx.enter_context(tc.tile_pool(name="npool", bufs=3))
@@ -61,7 +64,7 @@ def tile_layernormgrucell_pa_t_kernel(tc, x, h, W_r, U_r, W_c, U_c, ln_gamma, ln
         opool = ctx.enter_context(tc.tile_pool(name="opool", bufs=4))
         sm = ctx.enter_context(tc.tile_pool(name="sm", bufs=6))
         psV = ctx.enter_context(tc.psum_pool(name="psV", bufs=V_BUFS))
-        psT = ctx.enter_context(tc.psum_pool(name="psT", bufs=1))
+        psT = ctx.enter_context(tc.psum_pool(name="psT", bufs=T_BUFS))
 
         work = {"v": 0, "s": 0}
 
@@ -69,12 +72,10 @@ def tile_layernormgrucell_pa_t_kernel(tc, x, h, W_r, U_r, W_c, U_c, ln_gamma, ln
             work[eng] += cols + (FIX_V if eng == "v" else FIX_S)
 
         def pick(cols, force=False):
-            eng = "v" if force or work["v"] + FIX_V + BIAS < work["s"] + FIX_S else "s"
-            did(eng, cols)
-            return eng
+            return "v" if force else "s"
 
-        def evac(dst, src, cols):
-            if pick(cols) == "v":
+        def evac(dst, src, cols, on_scalar=False):
+            if not on_scalar:
                 nc.vector.tensor_copy(out=dst, in_=src)
             else:
                 nc.scalar.copy(out=dst, in_=src)
@@ -94,7 +95,7 @@ def tile_layernormgrucell_pa_t_kernel(tc, x, h, W_r, U_r, W_c, U_c, ln_gamma, ln
 
         ident = const.tile([P, P], F32, name="ident")
         make_identity(nc, ident[:])
-        mhalf = const.tile([P, 2], F32, name="mhalf")
+        mhalf = const.tile([P, 2 * GB], F32, name="mhalf")
         nc.gpsimd.memset(mhalf[:], -0.5)
         warm = const.tile([P, 1], F32, name="warm")
         nc.vector.memset(warm[:], 0.0)
@@ -134,15 +135,15 @@ def tile_layernormgrucell_pa_t_kernel(tc, x, h, W_r, U_r, W_c, U_c, ln_gamma, ln
                     nc.tensor.transpose(tp[:, u, oo * P:(oo + 1) * P], w32[:, u * P:(u + 1) * P], ident[:])
             return tp
 
-        def bank_to_group(dst, half, tp):
+        def bank_to_group(dst, half, tp, on_scalar=False):
             d32 = dst[:].bitcast(F32).rearrange("p (n u) -> p n u", u=2)
-            evac(d32[:, half * 256:(half + 1) * 256, :], tp[:].rearrange("p u n -> p n u"), D)
+            evac(d32[:, half * 256:(half + 1) * 256, :], tp[:].rearrange("p u n -> p n u"), D, on_scalar)
 
         def w_pe_ev(i, b, pool, tag):
             if b == 0:
-                gw = wp.tile([P, 4 * D], BF16, tag="gw", align_bytes=64)
+                gw = wp.tile([P, 4 * D], BF16, tag="gw", bufs=2, align_bytes=64)
                 wg[i] = gw
-            bank_to_group(wg[i], b, words_to_bank(pool, tag, wraw[i], 2 * b))
+            bank_to_group(wg[i], b, words_to_bank(pool, tag, wraw[i], 2 * b), b == 1)
 
         def w_q(i):
             quant(wq[i][:], ws[i][:], wg[i][:], 4 * D)
@@ -154,21 +155,21 @@ def tile_layernormgrucell_pa_t_kernel(tc, x, h, W_r, U_r, W_c, U_c, ln_gamma, ln
         gx = {}
         ptp = {}
 
-        def p_pe(s, k, pool=None, tag="tz"):
+        def p_pe(s, k, pool=None, tag="t"):
             if k == 0:
-                g_h = grp.tile([P, 4 * ST], BF16, tag="gh", bufs=5, align_bytes=64)
+                g_h = grp.tile([P, 4 * ST], BF16, tag="gh", bufs=6, align_bytes=64)
                 g_x = grp.tile([P, 4 * ST], BF16, tag="gx", align_bytes=64)
                 gh[s] = g_h
                 gx[s] = g_x
             ptp[(s, k)] = words_to_bank(pool or psT, tag, xh[s][k // 2], 2 * (k % 2))
 
         def p_ev(s, k):
-            bank_to_group(gh[s] if k < 2 else gx[s], k % 2, ptp[(s, k)])
+            bank_to_group(gh[s] if k < 2 else gx[s], k % 2, ptp[(s, k)], k in S_EVAC or (s == 0 and k % 2 == 1))
 
         def p_q(s, which):
             if which == 0:
-                hq_c = qp.tile([P, ST], U32, tag="hq", align_bytes=64)
-                hq_s = qp.tile([P, ST], U8, tag="hs", align_bytes=64)
+                hq_c = qp.tile([P, ST], U32, tag="hq", bufs=4, align_bytes=64)
+                hq_s = qp.tile([P, ST], U8, tag="hs", bufs=4, align_bytes=64)
                 quant(hq_c[:], hq_s[:], gh[s][:], 4 * ST)
                 hq[s] = (hq_c, hq_s)
             else:
@@ -178,7 +179,7 @@ def tile_layernormgrucell_pa_t_kernel(tc, x, h, W_r, U_r, W_c, U_c, ln_gamma, ln
             pr_str = pr32[:].rearrange("p (u q e) -> p u e q", u=2, e=2)
             res = []
             for kind in range(2):
-                tp = psT.tile([P, NT, P], F32, tag="tb")
+                tp = psT.tile([P, NT, P], F32, tag="t")
                 for t in range(NT):
                     src = pr_str[:, t // 2, t % 2, :] if kind == 0 else pr32[:, t * P:(t + 1) * P]
                     nc.tensor.transpose(tp[:, t, :], src, ident[:])
@@ -195,60 +196,72 @@ def tile_layernormgrucell_pa_t_kernel(tc, x, h, W_r, U_r, W_c, U_c, ln_gamma, ln
         vab = {}
         sca = {}
 
-        def a_pe(unit, j):
+        def mx_pair(unit, j):
             s, stage = unit
             js = slice(j * P, (j + 1) * P)
             a_c, a_s_ = hq[s] if stage == 1 else hrq[s]
             wa, wb = (0, 1) if stage == 1 else (2, 3)
             va = psV.tile([P, D], F32, tag="v")
+            nc.tensor.matmul_mx(out=va[:], lhsT=a_c[:, js].bitcast(FP8X4), lhsT_scale=a_s_[:, js],
+                                rhs=wq[wa][:].bitcast(FP8X4), rhs_scale=ws[wa][:], start=True, stop=True)
             vb = psV.tile([P, D], F32, tag="v")
-            for rep in range(MX_REP):
-                nc.tensor.matmul_mx(out=va[:], lhsT=a_c[:, js].bitcast(FP8X4), lhsT_scale=a_s_[:, js],
-                                    rhs=wq[wa][:].bitcast(FP8X4), rhs_scale=ws[wa][:], start=True, stop=True)
-                nc.tensor.matmul_mx(out=vb[:], lhsT=xq[:, s, js].bitcast(FP8X4), lhsT_scale=xs[:, s, js],
-                                    rhs=wq[wb][:].bitcast(FP8X4), rhs_scale=ws[wb][:], start=True, stop=True)
-            vab[(unit, j)] = (va, vb)
+            nc.tensor.matmul_mx(out=vb[:], lhsT=xq[:, s, js].bitcast(FP8X4), lhsT_scale=xs[:, s, js],
+                                rhs=wq[wb][:].bitcast(FP8X4), rhs_scale=ws[wb][:], start=True, stop=True)
+            return (va, vb)
 
-        def a_v(unit, j):
+        def a1_pe(unit, j):
+            vab[(unit, j)] = mx_pair(unit, j)
+
+        def a1_v(unit, j):
             va, vb = vab[(unit, j)]
             st = sm.tile([P, 2, 6], F32, tag="st")
             nc.vector.bn_stats(out=st[:, 0, :], in_=va[:])
             nc.vector.bn_stats(out=st[:, 1, :], in_=vb[:])
-            mv = sm.tile([P, 2, 2], F32, tag="mv")
-            nc.vector.bn_aggr(out=mv[:, 0, :], in_=st[:, 0, :])
-            nc.vector.bn_aggr(out=mv[:, 1, :], in_=st[:, 1, :])
+            jb = j // GB
+            if j % GB == 0:
+                mv = sm.tile([P, 2 * GB, 2], F32, tag="mv")
+                sca[(unit, jb)] = [mv, None, None]
+            mv = sca[(unit, jb)][0]
+            k = 2 * (j % GB)
+            nc.vector.bn_aggr(out=mv[:, k, :], in_=st[:, 0, :])
+            nc.vector.bn_aggr(out=mv[:, k + 1, :], in_=st[:, 1, :])
             did("v", D)
             did("v", D)
             did("v", 54)
             did("v", 54)
-            ve = sm.tile([P, 2], F32, tag="ve")
-            nc.gpsimd.tensor_scalar(out=ve[:], in0=mv[:, :, 1], scalar1=1.0, scalar2=EPS, op0=ALU.mult, op1=ALU.add)
-            rs = sm.tile([P, 2], F32, tag="rs")
-            nc.gpsimd.tensor_tensor(out=rs[:], in0=ve[:], in1=mhalf[:], op=ALU.pow)
-            mr = sm.tile([P, 2], F32, tag="mr")
-            nc.gpsimd.tensor_tensor(out=mr[:], in0=mv[:, :, 0], in1=rs[:], op=ALU.mult)
-            cc = sm.tile([P, 2], F32, tag="cc")
-            nc.gpsimd.tensor_scalar(out=cc[:], in0=mr[:], scalar1=-1.0, scalar2=0.0, op0=ALU.mult, op1=ALU.add)
-            sca[(unit, j)] = (rs, cc, mv)
+            if j % GB == GB - 1:
+                ve = sm.tile([P, 2 * GB], F32, tag="ve")
+                nc.gpsimd.tensor_scalar(out=ve[:], in0=mv[:, :, 1], scalar1=1.0, scalar2=EPS, op0=ALU.mult, op1=ALU.add)
+                rs = sm.tile([P, 2 * GB], F32, tag="rs")
+                nc.gpsimd.tensor_tensor(out=rs[:], in0=ve[:], in1=mhalf[:], op=ALU.pow)
+                mr = sm.tile([P, 2 * GB], F32, tag="mr")
+                nc.gpsimd.tensor_tensor(out=mr[:], in0=mv[:, :, 0], in1=rs[:], op=ALU.mult)
+                cc = sm.tile([P, 2 * GB], F32, tag="cc")
+                nc.gpsimd.tensor_scalar(out=cc[:], in0=mr[:], scalar1=-1.0, scalar2=0.0, op0=ALU.mult, op1=ALU.add)
+                sca[(unit, jb)][1] = rs
+                sca[(unit, jb)][2] = cc
 
-        def a_s(unit, j):
+        vn = {}
+
+        def a2_pe(unit, j):
+            vn[(unit, j)] = mx_pair(unit, j)
+
+        def a2(unit, j):
             if j == 0:
                 na = npool.tile([P, NJ, D], F32, tag="na")
                 nb = npool.tile([P, NJ, D], F32, tag="nb")
                 nab[unit] = (na, nb)
-            rs, cc, mv = sca[(unit, j)]
+            mv, rs, cc = sca[(unit, j // GB)]
             for w in range(2):
-                affine(nab[unit][w][:, j, :], vab[(unit, j)][w][:], rs[:, w:w + 1], cc[:, w:w + 1], mv[:, w, 0:1],
+                k = 2 * (j % GB) + w
+                affine(nab[unit][w][:, j, :], vn[(unit, j)][w][:], rs[:, k:k + 1], cc[:, k:k + 1], mv[:, k, 0:1],
                        4 * UNITS.index(unit) + j >= FORCE_A)
 
         tab_ = {}
 
         def b_pe(unit, t, which):
             src = nab[unit][which]
-            if UNITS.index(unit) == len(UNITS) - 1 and t % 2 == 1:
-                tt = psV.tile([P, ST], F32, tag="v")
-            else:
-                tt = psT.tile([P, ST], F32, tag="ta" if which == 0 else "tb", bufs=TA_BUFS if which == 0 else 1)
+            tt = psT.tile([P, ST], F32, tag="t")
             for j in range(NJ):
                 nc.tensor.transpose(tt[:, j * P:(j + 1) * P], src[:, j, t * P:(t + 1) * P], ident[:])
             tab_[(unit, t, which)] = tt
@@ -276,12 +289,7 @@ def tile_layernormgrucell_pa_t_kernel(tc, x, h, W_r, U_r, W_c, U_c, ln_gamma, ln
             if unit[1] == 1:
                 return
             zt = ztl[unit]
-            if UNITS.index(unit) >= len(UNITS) - 2 and i % 2 == 1:
-                zo = psV.tile([P, D], F32, tag="v")
-            elif UNITS.index(unit) == len(UNITS) - 1 and i == 2:
-                zo = psT.tile([P, D], F32, tag="ta")
-            else:
-                zo = psT.tile([P, D], F32, tag="tz")
+            zo = psT.tile([P, D], F32, tag="t")
             for t in range(NT):
                 nc.tensor.transpose(zo[:, t * P:(t + 1) * P], zt[:, t, i * P:(i + 1) * P], ident[:])
             zol[(unit, i)] = zo
@@ -324,8 +332,8 @@ def tile_layernormgrucell_pa_t_kernel(tc, x, h, W_r, U_r, W_c, U_c, ln_gamma, ln
             if stage != 1:
                 return
             if i == 0:
-                c_c = qp.tile([P, ST], U32, tag="hrq", bufs=4, align_bytes=64)
-                c_s_ = qp.tile([P, ST], U8, tag="hrs", bufs=4, align_bytes=64)
+                c_c = qp.tile([P, ST], U32, tag="hrq", bufs=5, align_bytes=64)
+                c_s_ = qp.tile([P, ST], U8, tag="hrs", bufs=5, align_bytes=64)
                 hrq[s] = (c_c, c_s_)
             c_c, c_s_ = hrq[s]
             rr = slice(i * P, (i + 1) * P)
@@ -341,7 +349,6 @@ def tile_layernormgrucell_pa_t_kernel(tc, x, h, W_r, U_r, W_c, U_c, ln_gamma, ln
         load(1)
         load_weight(2, W_c, False)
         load_weight(3, U_c, False)
-        load(2)
 
         n = len(UNITS)
         nslot = 4 * n
@@ -365,62 +372,57 @@ def tile_layernormgrucell_pa_t_kernel(tc, x, h, W_r, U_r, W_c, U_c, ln_gamma, ln
         p_pe(0, 1, psV, "v")
         p_ev(0, 1)
         w_q(0)
-        p_pe(0, 2, psT, "tb")
+        p_pe(0, 2)
         p_ev(0, 2)
-        p_pe(0, 3, psT, "tz")
+        p_pe(0, 3)
         p_ev(0, 3)
         p_q(0, 0)
-        w_pe_ev(1, 0, psT, "ta")
-        w_pe_ev(1, 1, psV, "v")
+        w_pe_ev(1, 0, psT, "t")
+        w_pe_ev(1, 1, psT, "t")
         p_q(0, 1)
         w_q(1)
         pr32 = const.tile([P, D], F32, name="pr32")
         nc.gpsimd.tensor_scalar(out=pr32[:], in0=pr_bf[:], scalar1=1.0, scalar2=0.0, op0=ALU.mult, op1=ALU.add)
-        run(a_pe, 0)
+        run(a1_pe, 0)
 
         tabs = []
-        for it in range(-1, nslot + LD + 2):
-            run(b_s, it - LBP - 1)
-            run(a_v, it)
-            run(a_s, it - LA)
-            run(b_v, it - LBP - 1)
-            run(c_s, it - LCP - 1)
-            run(d_v, it - LD)
-            run(d_q, it - LD - 1)
+        for it in range(-1, nslot + LD + 3):
+            tk = task(it - LB)
+            if tk is not None:
+                b_pe(tk[0], tk[1], 0)
+            run(c_pe, it - LC)
             for s in range(1, NST):
-                k = it - (first1[s] - LPREP[s]) - 1
-                tight = LPREP[s] < 6
+                k = it - (first1[s] - LPREP[s])
+                if 0 <= k < 4:
+                    p_pe(s, k)
+            if 1 <= it < 5:
+                w_pe_ev(2 + (it - 1) // 2, (it - 1) % 2, psT, "t")
+            if it == 5:
+                tabs.extend(prep_params())
+            if tk is not None:
+                b_pe(tk[0], tk[1], 1)
+            run(a2_pe, it - LN)
+            if it >= 1:
+                run(a1_pe, it)
+            run(b_s, it - LB)
+            run(c_s, it - LC)
+            run(a2, it - LN)
+            for s in range(1, NST):
+                k = it - (first1[s] - LPREP[s])
                 if 0 <= k < 4:
                     p_ev(s, k)
-                if k == (2 if tight else 3):
+                if k == 2:
                     p_q(s, 0)
-                if k == (3 if tight else 4):
+                if k == 4:
                     p_q(s, 1)
-            if it == 2:
+            if it == 3:
                 w_q(2)
-            if it == 4:
+            if it == 5:
                 w_q(3)
-            for what in PE_ORDER:
-                if what == "ta":
-                    tk = task(it - LBP)
-                    if tk is not None:
-                        b_pe(tk[0], tk[1], 0)
-                    if 0 <= it < 4:
-                        w_pe_ev(2 + it // 2, it % 2, psT, "ta")
-                if what == "tb":
-                    tk = task(it - LBP)
-                    if tk is not None:
-                        b_pe(tk[0], tk[1], 1)
-                    if it == 1:
-                        tabs.extend(prep_params())
-                if what == "mx" and it >= 0:
-                    run(a_pe, it + 1)
-                if what == "tz":
-                    run(c_pe, it - LCP)
-                    for s in range(1, NST):
-                        k = it - (first1[s] - LPREP[s])
-                        if 0 <= k < 4:
-                            p_pe(s, k)
-            for s in range(3, NST):
-                if it == max(first1[s] - LLOAD, -1 + 2 * (s - 3)):
+            run(d_q, it - LD - DQ)
+            run(d_v, it - LD)
+            run(b_v, it - LB)
+            run(a1_v, it)
+            for s in range(2, NST):
+                if it == max(first1[s] - LPREP[s] - LLOAD, -1):
                     load(s)

@@ -21,28 +21,27 @@ NT = D // P
 EPS = 1e-5
 FLOPS = 4 * 2 * ROWS * D * D
 
-MANUAL = True
-UNITS = [(0, 1), (1, 1), (2, 1), (3, 1), (4, 1), (0, 2), (5, 1), (1, 2), (6, 1), (2, 2), (7, 1), (3, 2),
-         (4, 2), (5, 2), (6, 2), (7, 2)]
-GB = 2
-LN = 4
-LB = LN + 5
-LC = LB + 4
-LD = LC + 4
-LPREP = [0, 5, 5, 5, 5, 8, 8, 8]
-DQ = 2
-S_EVAC = [3]
-LLOAD = 3
-V_BUFS = 4
-T_BUFS = 4
-PE_ORDER = ["ta", "tb", "tz", "mx"]
+CHAIN = 2
+NORM_LAG = 4
+GAIN_LAG = NORM_LAG + 5
+ACT_LAG = GAIN_LAG + 4
+MUL_LAG = ACT_LAG + 4
+QUANT_LAG = MUL_LAG + 2
+STAGE_GAP = 5
+INPUT_LEAD = 5
+LOAD_LEAD = 3
+LATE_WEIGHTS = 10
+GAIN_TABLES = 5
+SCALAR_COPIES_UPTO = 2
+VECTOR_NORMS_LAST_UNITS = 4
 G_ROWS = 64
-FIX_V = 18
-FIX_S = 60
-BIAS = 0
-EVAC_V = True
-FORCE_A = 62
-FORCE_B = 60
+
+
+def unit_order():
+    order = [(s, 1) for s in range(STAGE_GAP)]
+    for s in range(NST - STAGE_GAP):
+        order += [(s, 2), (s + STAGE_GAP, 1)]
+    return order + [(s, 2) for s in range(NST - STAGE_GAP, NST)]
 
 
 def tile_layernormgrucell_pa_t_kernel(tc, x, h, W_r, U_r, W_c, U_c, ln_gamma, ln_beta, out):
@@ -50,379 +49,340 @@ def tile_layernormgrucell_pa_t_kernel(tc, x, h, W_r, U_r, W_c, U_c, ln_gamma, ln
     x_v = x.rearrange("(s j p) k -> p s j k", s=NST, j=NJ)
     h_v = h.rearrange("(s j p) k -> p s j k", s=NST, j=NJ)
     out_v = out.rearrange("(s j p) f -> p s j f", s=NST, j=NJ)
+    units = unit_order()
+    slots = NJ * len(units)
+    first_slot = {s: NJ * units.index((s, 1)) for s in range(NST)}
 
     with ExitStack() as ctx:
-        if MANUAL:
-            ctx.enter_context(tc.manual_schedule())
+        ctx.enter_context(tc.manual_schedule())
         const = ctx.enter_context(tc.tile_pool(name="const", bufs=1))
-        wp = ctx.enter_context(tc.tile_pool(name="wp", bufs=2))
+        wpool = ctx.enter_context(tc.tile_pool(name="wpool", bufs=2))
         io = ctx.enter_context(tc.tile_pool(name="io", bufs=2))
-        grp = ctx.enter_context(tc.tile_pool(name="grp", bufs=2))
-        qp = ctx.enter_context(tc.tile_pool(name="qp", bufs=3))
-        npool = ctx.enter_context(tc.tile_pool(name="npool", bufs=3))
-        zpool = ctx.enter_context(tc.tile_pool(name="zpool", bufs=4))
-        opool = ctx.enter_context(tc.tile_pool(name="opool", bufs=4))
-        sm = ctx.enter_context(tc.tile_pool(name="sm", bufs=6))
-        psV = ctx.enter_context(tc.psum_pool(name="psV", bufs=V_BUFS))
-        psT = ctx.enter_context(tc.psum_pool(name="psT", bufs=T_BUFS))
-
-        work = {"v": 0, "s": 0}
-
-        def did(eng, cols):
-            work[eng] += cols + (FIX_V if eng == "v" else FIX_S)
-
-        def pick(cols, force=False):
-            return "v" if force else "s"
-
-        def evac(dst, src, cols, on_scalar=False):
-            if not on_scalar:
-                nc.vector.tensor_copy(out=dst, in_=src)
-            else:
-                nc.scalar.copy(out=dst, in_=src)
-
-        def affine(dst, src, mul, add, sub_first, force):
-            if pick(D, force) == "v":
-                if sub_first is None:
-                    nc.vector.tensor_scalar(out=dst, in0=src, scalar1=mul, scalar2=add, op0=ALU.mult, op1=ALU.add)
-                else:
-                    nc.vector.tensor_scalar(out=dst, in0=src, scalar1=sub_first, scalar2=mul, op0=ALU.subtract, op1=ALU.mult)
-            else:
-                nc.scalar.activation(out=dst, in_=src, func=ACT.Identity, bias=add, scale=mul)
-
-        def quant(codes, scales, src, cols):
-            nc.vector.quantize_mx(out=codes.bitcast(FP8X4), scales=scales, in_=src)
-            did("v", cols // 4)
+        words = ctx.enter_context(tc.tile_pool(name="words", bufs=2))
+        codes = ctx.enter_context(tc.tile_pool(name="codes", bufs=4))
+        normed = ctx.enter_context(tc.tile_pool(name="normed", bufs=3))
+        sums = ctx.enter_context(tc.tile_pool(name="sums", bufs=4))
+        outs = ctx.enter_context(tc.tile_pool(name="outs", bufs=4))
+        small = ctx.enter_context(tc.tile_pool(name="small", bufs=6))
+        mx_banks = ctx.enter_context(tc.psum_pool(name="mx_banks", bufs=4))
+        tr_banks = ctx.enter_context(tc.psum_pool(name="tr_banks", bufs=4))
 
         ident = const.tile([P, P], F32, name="ident")
         make_identity(nc, ident[:])
-        mhalf = const.tile([P, 2 * GB], F32, name="mhalf")
-        nc.gpsimd.memset(mhalf[:], -0.5)
+        minus_half = const.tile([P, 2 * CHAIN], F32, name="minus_half")
+        nc.gpsimd.memset(minus_half[:], -0.5)
         warm = const.tile([P, 1], F32, name="warm")
         nc.vector.memset(warm[:], 0.0)
         nc.scalar.activation(out=warm[:], in_=warm[:], func=ACT.Sigmoid)
 
-        xh = {}
+        def words_to_bank(pool, src, first):
+            bank = pool.tile([P, 2, 2 * P], F32, tag="bank")
+            for i in range(2):
+                src32 = src[:, first + i, :].bitcast(F32)
+                for u in range(2):
+                    nc.tensor.transpose(bank[:, u, i * P:(i + 1) * P], src32[:, u * P:(u + 1) * P], ident[:])
+            return bank
 
-        def load(s):
+        def bank_to_words(dst, half, bank, on_scalar):
+            dst32 = dst[:].bitcast(F32).rearrange("p (n u) -> p n u", u=2)[:, half * 2 * P:(half + 1) * 2 * P, :]
+            if on_scalar:
+                nc.scalar.copy(out=dst32, in_=bank[:].rearrange("p u n -> p n u"))
+            else:
+                nc.vector.tensor_copy(out=dst32, in_=bank[:].rearrange("p u n -> p n u"))
+
+        def quantise(code_words, scales, src):
+            nc.vector.quantize_mx(out=code_words.bitcast(FP8X4), scales=scales, in_=src)
+
+        w_raw = {}
+        w_words = {}
+        w_codes = [const.tile([P, D], U32, name="w_codes%d" % i, align_bytes=64) for i in range(4)]
+        w_scales = [const.tile([P, D], U8, name="w_scales%d" % i, align_bytes=64) for i in range(4)]
+
+        def load_weight(i, w):
+            raw = wpool.tile([P, NT, D], BF16, tag="raw", bufs=4)
+            if i < 2:
+                nc.sync.dma_start(out=raw[:].rearrange("p (u e) k -> p u e k", u=2),
+                                  in_=w.rearrange("(u p e) k -> p u e k", u=2, e=2))
+            else:
+                nc.sync.dma_start(out=raw[:], in_=w.rearrange("(t p) k -> p t k", p=P))
+            w_raw[i] = raw
+
+        def weight_words(i, half, pool):
+            if half == 0:
+                grouped = wpool.tile([P, 4 * D], BF16, tag="grouped", align_bytes=64)
+                w_words[i] = grouped
+            bank_to_words(w_words[i], half, words_to_bank(pool, w_raw[i], 2 * half), half == 1)
+
+        def quantise_weight(i):
+            quantise(w_codes[i][:], w_scales[i][:], w_words[i][:])
+
+        rows_in = {}
+        h_words = {}
+        x_words = {}
+        in_banks = {}
+        h_codes = {}
+        x_codes = const.tile([P, NST, ST], U32, name="x_codes", align_bytes=64)
+        x_scales = const.tile([P, NST, ST], U8, name="x_scales", align_bytes=64)
+
+        def load_rows(s):
             h_sb = io.tile([P, NJ, D], BF16, tag="h_sb")
             nc.sync.dma_start(out=h_sb[:], in_=h_v[:, s])
             x_sb = io.tile([P, NJ, D], BF16, tag="x_sb")
             nc.sync.dma_start(out=x_sb[:], in_=x_v[:, s])
-            xh[s] = (h_sb, x_sb)
+            rows_in[s] = (h_sb, x_sb)
 
-        wraw = {}
+        def input_transposes(s, piece, pool):
+            if piece == 0:
+                h_w = words.tile([P, 4 * ST], BF16, tag="h_w", bufs=6, align_bytes=64)
+                x_w = words.tile([P, 4 * ST], BF16, tag="x_w", align_bytes=64)
+                h_words[s] = h_w
+                x_words[s] = x_w
+            in_banks[(s, piece)] = words_to_bank(pool, rows_in[s][piece // 2], 2 * (piece % 2))
 
-        def load_weight(i, w_ap, permuted):
-            raw = wp.tile([P, NT, D], BF16, tag="wraw", bufs=4)
-            if permuted:
-                nc.sync.dma_start(
-                    out=raw[:].rearrange("p (u e) k -> p u e k", u=2),
-                    in_=w_ap.rearrange("(u p e) k -> p u e k", u=2, e=2),
-                )
-            else:
-                nc.sync.dma_start(out=raw[:], in_=w_ap.rearrange("(t p) k -> p t k", p=P))
-            wraw[i] = raw
+        def input_copy(s, piece):
+            on_scalar = piece % 2 == 1 if s == 0 else s <= SCALAR_COPIES_UPTO
+            bank_to_words(h_words[s] if piece < 2 else x_words[s], piece % 2, in_banks[(s, piece)], on_scalar)
 
-        wq = [const.tile([P, D], U32, name="wq%d" % i, align_bytes=64) for i in range(4)]
-        ws = [const.tile([P, D], U8, name="ws%d" % i, align_bytes=64) for i in range(4)]
-        wg = {}
+        def quantise_h(s):
+            c_w = codes.tile([P, ST], U32, tag="h_codes", align_bytes=64)
+            c_s = codes.tile([P, ST], U8, tag="h_scales", align_bytes=64)
+            quantise(c_w[:], c_s[:], h_words[s][:])
+            h_codes[s] = (c_w, c_s)
 
-        def words_to_bank(pool, tag, src, first):
-            tp = pool.tile([P, 2, 256], F32, tag=tag)
-            for oo in range(2):
-                w32 = src[:, first + oo, :].bitcast(F32)
-                for u in range(2):
-                    nc.tensor.transpose(tp[:, u, oo * P:(oo + 1) * P], w32[:, u * P:(u + 1) * P], ident[:])
-            return tp
+        def quantise_x(s):
+            quantise(x_codes[:, s, :], x_scales[:, s, :], x_words[s][:])
 
-        def bank_to_group(dst, half, tp, on_scalar=False):
-            d32 = dst[:].bitcast(F32).rearrange("p (n u) -> p n u", u=2)
-            evac(d32[:, half * 256:(half + 1) * 256, :], tp[:].rearrange("p u n -> p n u"), D, on_scalar)
-
-        def w_pe_ev(i, b, pool, tag):
-            if b == 0:
-                gw = wp.tile([P, 4 * D], BF16, tag="gw", bufs=2, align_bytes=64)
-                wg[i] = gw
-            bank_to_group(wg[i], b, words_to_bank(pool, tag, wraw[i], 2 * b), b == 1)
-
-        def w_q(i):
-            quant(wq[i][:], ws[i][:], wg[i][:], 4 * D)
-
-        xq = const.tile([P, NST, ST], U32, name="xq", align_bytes=64)
-        xs = const.tile([P, NST, ST], U8, name="xs", align_bytes=64)
-        hq = {}
-        gh = {}
-        gx = {}
-        ptp = {}
-
-        def p_pe(s, k, pool=None, tag="t"):
-            if k == 0:
-                g_h = grp.tile([P, 4 * ST], BF16, tag="gh", bufs=6, align_bytes=64)
-                g_x = grp.tile([P, 4 * ST], BF16, tag="gx", align_bytes=64)
-                gh[s] = g_h
-                gx[s] = g_x
-            ptp[(s, k)] = words_to_bank(pool or psT, tag, xh[s][k // 2], 2 * (k % 2))
-
-        def p_ev(s, k):
-            bank_to_group(gh[s] if k < 2 else gx[s], k % 2, ptp[(s, k)], k in S_EVAC or (s == 0 and k % 2 == 1))
-
-        def p_q(s, which):
-            if which == 0:
-                hq_c = qp.tile([P, ST], U32, tag="hq", bufs=4, align_bytes=64)
-                hq_s = qp.tile([P, ST], U8, tag="hs", bufs=4, align_bytes=64)
-                quant(hq_c[:], hq_s[:], gh[s][:], 4 * ST)
-                hq[s] = (hq_c, hq_s)
-            else:
-                quant(xq[:, s, :], xs[:, s, :], gx[s][:], 4 * ST)
-
-        def prep_params():
-            pr_str = pr32[:].rearrange("p (u q e) -> p u e q", u=2, e=2)
-            res = []
-            for kind in range(2):
-                tp = psT.tile([P, NT, P], F32, tag="t")
+        def gain_tables():
+            strided = params32[:].rearrange("p (u q e) -> p u e q", u=2, e=2)
+            tables = []
+            for stage in (1, 2):
+                bank = tr_banks.tile([P, NT, P], F32, tag="bank")
                 for t in range(NT):
-                    src = pr_str[:, t // 2, t % 2, :] if kind == 0 else pr32[:, t * P:(t + 1) * P]
-                    nc.tensor.transpose(tp[:, t, :], src, ident[:])
-                tab = const.tile([P, 8, NT], F32, name="prm%d" % kind)
-                nc.vector.tensor_copy(out=tab[:], in_=tp[:, :, 0:8].rearrange("p c i -> p i c"))
-                bs = const.tile([P, NT], F32, name="bs%d" % kind)
-                nc.vector.tensor_tensor(out=bs[:], in0=tab[:, 4 + 2 * kind, :], in1=tab[:, 5 + 2 * kind, :], op=ALU.add)
-                res.append((tab, bs))
-            return res
+                    chunk = strided[:, t // 2, t % 2, :] if stage == 1 else params32[:, t * P:(t + 1) * P]
+                    nc.tensor.transpose(bank[:, t, :], chunk, ident[:])
+                table = const.tile([P, 8, NT], F32, name="table%d" % stage)
+                nc.vector.tensor_copy(out=table[:], in_=bank[:, :, 0:8].rearrange("p c i -> p i c"))
+                bias = const.tile([P, NT], F32, name="bias%d" % stage)
+                nc.vector.tensor_tensor(out=bias[:], in0=table[:, 2 + 2 * stage, :], in1=table[:, 3 + 2 * stage, :],
+                                        op=ALU.add)
+                tables.append((table, bias))
+            return tables
 
-        nab = {}
-        ztl = {}
-        hrq = {}
-        vab = {}
-        sca = {}
+        hr_codes = {}
+        stat_banks = {}
+        stat_parts = {}
+        moments = {}
 
-        def mx_pair(unit, j):
+        def products(unit, j):
             s, stage = unit
-            js = slice(j * P, (j + 1) * P)
-            a_c, a_s_ = hq[s] if stage == 1 else hrq[s]
-            wa, wb = (0, 1) if stage == 1 else (2, 3)
-            va = psV.tile([P, D], F32, tag="v")
-            nc.tensor.matmul_mx(out=va[:], lhsT=a_c[:, js].bitcast(FP8X4), lhsT_scale=a_s_[:, js],
-                                rhs=wq[wa][:].bitcast(FP8X4), rhs_scale=ws[wa][:], start=True, stop=True)
-            vb = psV.tile([P, D], F32, tag="v")
-            nc.tensor.matmul_mx(out=vb[:], lhsT=xq[:, s, js].bitcast(FP8X4), lhsT_scale=xs[:, s, js],
-                                rhs=wq[wb][:].bitcast(FP8X4), rhs_scale=ws[wb][:], start=True, stop=True)
-            return (va, vb)
+            cols = slice(j * P, (j + 1) * P)
+            a_w, a_s = h_codes[s] if stage == 1 else hr_codes[s]
+            pair = []
+            for lhs_w, lhs_s, i in ((a_w[:, cols], a_s[:, cols], 2 * stage - 2),
+                                    (x_codes[:, s, cols], x_scales[:, s, cols], 2 * stage - 1)):
+                bank = mx_banks.tile([P, D], F32, tag="bank")
+                nc.tensor.matmul_mx(out=bank[:], lhsT=lhs_w.bitcast(FP8X4), lhsT_scale=lhs_s,
+                                    rhs=w_codes[i][:].bitcast(FP8X4), rhs_scale=w_scales[i][:], start=True, stop=True)
+                pair.append(bank)
+            return pair
 
-        def a1_pe(unit, j):
-            vab[(unit, j)] = mx_pair(unit, j)
+        def products_for_statistics(unit, j):
+            stat_banks[(unit, j)] = products(unit, j)
 
-        def a1_v(unit, j):
-            va, vb = vab[(unit, j)]
-            st = sm.tile([P, 2, 6], F32, tag="st")
-            nc.vector.bn_stats(out=st[:, 0, :], in_=va[:])
-            nc.vector.bn_stats(out=st[:, 1, :], in_=vb[:])
-            jb = j // GB
-            if j % GB == 0:
-                mv = sm.tile([P, 2 * GB, 2], F32, tag="mv")
-                sca[(unit, jb)] = [mv, None, None]
-            mv = sca[(unit, jb)][0]
-            k = 2 * (j % GB)
-            nc.vector.bn_aggr(out=mv[:, k, :], in_=st[:, 0, :])
-            nc.vector.bn_aggr(out=mv[:, k + 1, :], in_=st[:, 1, :])
-            did("v", D)
-            did("v", D)
-            did("v", 54)
-            did("v", 54)
-            if j % GB == GB - 1:
-                ve = sm.tile([P, 2 * GB], F32, tag="ve")
-                nc.gpsimd.tensor_scalar(out=ve[:], in0=mv[:, :, 1], scalar1=1.0, scalar2=EPS, op0=ALU.mult, op1=ALU.add)
-                rs = sm.tile([P, 2 * GB], F32, tag="rs")
-                nc.gpsimd.tensor_tensor(out=rs[:], in0=ve[:], in1=mhalf[:], op=ALU.pow)
-                mr = sm.tile([P, 2 * GB], F32, tag="mr")
-                nc.gpsimd.tensor_tensor(out=mr[:], in0=mv[:, :, 0], in1=rs[:], op=ALU.mult)
-                cc = sm.tile([P, 2 * GB], F32, tag="cc")
-                nc.gpsimd.tensor_scalar(out=cc[:], in0=mr[:], scalar1=-1.0, scalar2=0.0, op0=ALU.mult, op1=ALU.add)
-                sca[(unit, jb)][1] = rs
-                sca[(unit, jb)][2] = cc
+        def statistics(unit, j):
+            parts = small.tile([P, 2, 6], F32, tag="parts")
+            for side in range(2):
+                nc.vector.bn_stats(out=parts[:, side, :], in_=stat_banks[(unit, j)][side][:])
+            stat_parts[(unit, j)] = parts
 
-        vn = {}
+        def finish_statistics(unit, j):
+            k = 2 * (j % CHAIN)
+            if k == 0:
+                mean_var = small.tile([P, 2 * CHAIN, 2], F32, tag="mean_var")
+                moments[(unit, j // CHAIN)] = [mean_var]
+            mean_var = moments[(unit, j // CHAIN)][0]
+            for side in range(2):
+                nc.vector.bn_aggr(out=mean_var[:, k + side, :], in_=stat_parts[(unit, j)][:, side, :])
+            if j % CHAIN == CHAIN - 1:
+                var_eps = small.tile([P, 2 * CHAIN], F32, tag="var_eps")
+                nc.gpsimd.tensor_scalar(out=var_eps[:], in0=mean_var[:, :, 1], scalar1=1.0, scalar2=EPS,
+                                        op0=ALU.mult, op1=ALU.add)
+                rstd = small.tile([P, 2 * CHAIN], F32, tag="rstd")
+                nc.gpsimd.tensor_tensor(out=rstd[:], in0=var_eps[:], in1=minus_half[:], op=ALU.pow)
+                mean_rstd = small.tile([P, 2 * CHAIN], F32, tag="mean_rstd")
+                nc.gpsimd.tensor_tensor(out=mean_rstd[:], in0=mean_var[:, :, 0], in1=rstd[:], op=ALU.mult)
+                shift = small.tile([P, 2 * CHAIN], F32, tag="shift")
+                nc.gpsimd.tensor_scalar(out=shift[:], in0=mean_rstd[:], scalar1=-1.0, scalar2=0.0,
+                                        op0=ALU.mult, op1=ALU.add)
+                moments[(unit, j // CHAIN)] += [rstd, shift]
 
-        def a2_pe(unit, j):
-            vn[(unit, j)] = mx_pair(unit, j)
+        norm_banks = {}
+        normal = {}
 
-        def a2(unit, j):
-            if j == 0:
-                na = npool.tile([P, NJ, D], F32, tag="na")
-                nb = npool.tile([P, NJ, D], F32, tag="nb")
-                nab[unit] = (na, nb)
-            mv, rs, cc = sca[(unit, j // GB)]
-            for w in range(2):
-                k = 2 * (j % GB) + w
-                affine(nab[unit][w][:, j, :], vn[(unit, j)][w][:], rs[:, k:k + 1], cc[:, k:k + 1], mv[:, k, 0:1],
-                       4 * UNITS.index(unit) + j >= FORCE_A)
+        def products_to_normalise(unit, j):
+            norm_banks[(unit, j)] = products(unit, j)
 
-        tab_ = {}
+        def on_vector(unit, j, side):
+            return side == 1 and j % 2 == 1 and units.index(unit) >= len(units) - VECTOR_NORMS_LAST_UNITS
 
-        def b_pe(unit, t, which):
-            src = nab[unit][which]
-            tt = psT.tile([P, ST], F32, tag="t")
+        def normalise(unit, j, vector_turn):
+            if j == 0 and not vector_turn:
+                n_a = normed.tile([P, NJ, D], F32, tag="n_a")
+                n_b = normed.tile([P, NJ, D], F32, tag="n_b")
+                normal[unit] = (n_a, n_b)
+            mean_var, rstd, shift = moments[(unit, j // CHAIN)]
+            for side in range(2):
+                k = 2 * (j % CHAIN) + side
+                if on_vector(unit, j, side) != vector_turn:
+                    continue
+                if vector_turn:
+                    nc.vector.tensor_scalar(out=normal[unit][side][:, j, :], in0=norm_banks[(unit, j)][side][:],
+                                            scalar1=mean_var[:, k, 0:1], scalar2=rstd[:, k:k + 1],
+                                            op0=ALU.subtract, op1=ALU.mult)
+                else:
+                    nc.scalar.activation(out=normal[unit][side][:, j, :], in_=norm_banks[(unit, j)][side][:],
+                                         func=ACT.Identity, bias=shift[:, k:k + 1], scale=rstd[:, k:k + 1])
+
+        def normalise_on_scalar(unit, j):
+            normalise(unit, j, False)
+
+        def normalise_on_vector(unit, j):
+            normalise(unit, j, True)
+
+        feat_banks = {}
+        summed = {}
+
+        def to_features(unit, t, side):
+            bank = tr_banks.tile([P, ST], F32, tag="bank")
             for j in range(NJ):
-                nc.tensor.transpose(tt[:, j * P:(j + 1) * P], src[:, j, t * P:(t + 1) * P], ident[:])
-            tab_[(unit, t, which)] = tt
+                nc.tensor.transpose(bank[:, j * P:(j + 1) * P], normal[unit][side][:, j, t * P:(t + 1) * P], ident[:])
+            feat_banks[(unit, t, side)] = bank
 
-        def b_s(unit, t):
-            stage = unit[1]
+        def first_gain(unit, t):
             if t == 0:
-                zt = zpool.tile([P, NT, ST], F32, tag="zt")
-                ztl[unit] = zt
-            tab, bs = tabs[stage - 1]
-            affine(ztl[unit][:, t, :], tab_[(unit, t, 0)][:], tab[:, 2 * stage - 2, t:t + 1], bs[:, t:t + 1], None,
-                   4 * UNITS.index(unit) + t >= FORCE_B)
+                z = sums.tile([P, NT, ST], F32, tag="z")
+                summed[unit] = z
+            table, bias = tables[unit[1] - 1]
+            nc.scalar.activation(out=summed[unit][:, t, :], in_=feat_banks[(unit, t, 0)][:], func=ACT.Identity,
+                                 bias=bias[:, t:t + 1], scale=table[:, 2 * unit[1] - 2, t:t + 1])
 
-        def b_v(unit, t):
-            stage = unit[1]
-            tab, bs = tabs[stage - 1]
-            zt = ztl[unit]
-            nc.vector.scalar_tensor_tensor(out=zt[:, t, :], in0=tab_[(unit, t, 1)][:], scalar=tab[:, 2 * stage - 1, t:t + 1],
-                                           in1=zt[:, t, :], op0=ALU.mult, op1=ALU.add)
-            did("v", ST)
+        def second_gain(unit, t):
+            table, bias = tables[unit[1] - 1]
+            z = summed[unit]
+            nc.vector.scalar_tensor_tensor(out=z[:, t, :], in0=feat_banks[(unit, t, 1)][:],
+                                           scalar=table[:, 2 * unit[1] - 1, t:t + 1], in1=z[:, t, :],
+                                           op0=ALU.mult, op1=ALU.add)
 
-        zol = {}
+        row_banks = {}
 
-        def c_pe(unit, i):
+        def to_rows(unit, i):
+            if unit[1] == 2:
+                bank = tr_banks.tile([P, D], F32, tag="bank")
+                for t in range(NT):
+                    nc.tensor.transpose(bank[:, t * P:(t + 1) * P], summed[unit][:, t, i * P:(i + 1) * P], ident[:])
+                row_banks[(unit, i)] = bank
+
+        def activate(unit, i):
             if unit[1] == 1:
-                return
-            zt = ztl[unit]
-            zo = psT.tile([P, D], F32, tag="t")
-            for t in range(NT):
-                nc.tensor.transpose(zo[:, t * P:(t + 1) * P], zt[:, t, i * P:(i + 1) * P], ident[:])
-            zol[(unit, i)] = zo
-
-        def c_s(unit, i):
-            s, stage = unit
-            zt = ztl[unit]
-            did("s", D)
-            if stage == 1:
-                nc.scalar.activation(out=zt[:, i, :], in_=zt[:, i, :], func=ACT.Sigmoid)
+                nc.scalar.activation(out=summed[unit][:, i, :], in_=summed[unit][:, i, :], func=ACT.Sigmoid)
             else:
-                o_sb = opool.tile([P, D], F32, tag="o")
-                nc.scalar.activation(out=o_sb[:], in_=zol[(unit, i)][:], func=ACT.Tanh)
-                nc.sync.dma_start(out=out_v[:, s, i, :], in_=o_sb[:])
+                c_sb = outs.tile([P, D], F32, tag="c_sb")
+                nc.scalar.activation(out=c_sb[:], in_=row_banks[(unit, i)][:], func=ACT.Tanh)
+                nc.sync.dma_start(out=out_v[:, unit[0], i, :], in_=c_sb[:])
 
-        ghr = {}
+        hr_words = {}
 
-        def d_v(unit, i):
+        def multiply(unit, i):
             s, stage = unit
-            if stage != 1:
-                return
-            zt = ztl[unit]
-            if i == 0:
-                g_hr = grp.tile([P, 4 * ST], BF16, tag="ghr", align_bytes=64)
-                ghr[s] = g_hr
-            for eng, lo, hi in ((nc.gpsimd, 0, G_ROWS), (nc.vector, G_ROWS, P)):
-                if hi > lo:
-                    rr = slice(i * P + lo, i * P + hi)
-                    eng.tensor_tensor(
-                        out=ghr[s][:].rearrange("p (r t) -> p r t", t=4)[:, rr, :],
-                        in0=zt[:, :, rr].rearrange("p t r -> p r t"),
-                        in1=gh[s][:].rearrange("p (r t) -> p r t", t=4)[:, rr, :],
-                        op=ALU.mult,
-                    )
-            if G_ROWS < P:
-                did("v", 4 * (P - G_ROWS))
-
-        def d_q(unit, i):
-            s, stage = unit
-            if stage != 1:
+            if stage == 2:
                 return
             if i == 0:
-                c_c = qp.tile([P, ST], U32, tag="hrq", bufs=5, align_bytes=64)
-                c_s_ = qp.tile([P, ST], U8, tag="hrs", bufs=5, align_bytes=64)
-                hrq[s] = (c_c, c_s_)
-            c_c, c_s_ = hrq[s]
-            rr = slice(i * P, (i + 1) * P)
-            quant(c_c[:, rr], c_s_[:, rr], ghr[s][:, i * 4 * P:(i + 1) * 4 * P], 4 * P)
+                hr_w = words.tile([P, 4 * ST], BF16, tag="hr_w", align_bytes=64)
+                hr_words[s] = hr_w
+            for engine, lo, hi in ((nc.gpsimd, 0, G_ROWS), (nc.vector, G_ROWS, P)):
+                rows = slice(i * P + lo, i * P + hi)
+                engine.tensor_tensor(out=hr_words[s][:].rearrange("p (r t) -> p r t", t=4)[:, rows, :],
+                                     in0=summed[unit][:, :, rows].rearrange("p t r -> p r t"),
+                                     in1=h_words[s][:].rearrange("p (r t) -> p r t", t=4)[:, rows, :], op=ALU.mult)
 
-        load_weight(0, W_r, True)
-        load(0)
-        load_weight(1, U_r, True)
-        pr_bf = const.tile([P, D], BF16, name="pr_bf")
-        nc.vector.memset(pr_bf[:], 0.0)
-        nc.sync.dma_start(out=pr_bf[0:4, :], in_=ln_gamma)
-        nc.sync.dma_start(out=pr_bf[4:8, :], in_=ln_beta)
-        load(1)
-        load_weight(2, W_c, False)
-        load_weight(3, U_c, False)
+        def quantise_hr(unit, i):
+            s, stage = unit
+            if stage == 2:
+                return
+            if i == 0:
+                c_w = codes.tile([P, ST], U32, tag="hr_codes", bufs=5, align_bytes=64)
+                c_s = codes.tile([P, ST], U8, tag="hr_scales", bufs=5, align_bytes=64)
+                hr_codes[s] = (c_w, c_s)
+            c_w, c_s = hr_codes[s]
+            quantise(c_w[:, i * P:(i + 1) * P], c_s[:, i * P:(i + 1) * P], hr_words[s][:, i * 4 * P:(i + 1) * 4 * P])
 
-        n = len(UNITS)
-        nslot = 4 * n
-        first1 = {}
-        for u in range(n):
-            if UNITS[u][1] == 1:
-                first1[UNITS[u][0]] = 4 * u
+        def run(step, slot):
+            if 0 <= slot < slots:
+                step(units[slot // NJ], slot % NJ)
 
-        def task(k):
-            return (UNITS[k // 4], k % 4) if 0 <= k < nslot else None
+        load_weight(0, W_r)
+        load_rows(0)
+        load_weight(1, U_r)
+        params = const.tile([P, D], BF16, name="params")
+        nc.vector.memset(params[:], 0.0)
+        nc.sync.dma_start(out=params[0:4, :], in_=ln_gamma)
+        nc.sync.dma_start(out=params[4:8, :], in_=ln_beta)
+        load_rows(1)
+        load_weight(2, W_c)
+        load_weight(3, U_c)
 
-        def run(fn, k):
-            tk = task(k)
-            if tk is not None:
-                fn(tk[0], tk[1])
+        weight_words(0, 0, mx_banks)
+        weight_words(0, 1, mx_banks)
+        for piece in range(4):
+            input_transposes(0, piece, mx_banks if piece < 2 else tr_banks)
+            input_copy(0, piece)
+            if piece == 1:
+                quantise_weight(0)
+        quantise_h(0)
+        weight_words(1, 0, tr_banks)
+        weight_words(1, 1, tr_banks)
+        quantise_x(0)
+        quantise_weight(1)
+        params32 = const.tile([P, D], F32, name="params32")
+        nc.gpsimd.tensor_scalar(out=params32[:], in0=params[:], scalar1=1.0, scalar2=0.0, op0=ALU.mult, op1=ALU.add)
+        run(products_for_statistics, 0)
 
-        w_pe_ev(0, 0, psV, "v")
-        w_pe_ev(0, 1, psV, "v")
-        p_pe(0, 0, psV, "v")
-        p_ev(0, 0)
-        p_pe(0, 1, psV, "v")
-        p_ev(0, 1)
-        w_q(0)
-        p_pe(0, 2)
-        p_ev(0, 2)
-        p_pe(0, 3)
-        p_ev(0, 3)
-        p_q(0, 0)
-        w_pe_ev(1, 0, psT, "t")
-        w_pe_ev(1, 1, psT, "t")
-        p_q(0, 1)
-        w_q(1)
-        pr32 = const.tile([P, D], F32, name="pr32")
-        nc.gpsimd.tensor_scalar(out=pr32[:], in0=pr_bf[:], scalar1=1.0, scalar2=0.0, op0=ALU.mult, op1=ALU.add)
-        run(a1_pe, 0)
-
-        tabs = []
-        for it in range(-1, nslot + LD + 3):
-            tk = task(it - LB)
-            if tk is not None:
-                b_pe(tk[0], tk[1], 0)
-            run(c_pe, it - LC)
-            for s in range(1, NST):
-                k = it - (first1[s] - LPREP[s])
-                if 0 <= k < 4:
-                    p_pe(s, k)
-            if 1 <= it < 5:
-                w_pe_ev(2 + (it - 1) // 2, (it - 1) % 2, psT, "t")
-            if it == 5:
-                tabs.extend(prep_params())
-            if tk is not None:
-                b_pe(tk[0], tk[1], 1)
-            run(a2_pe, it - LN)
+        tables = []
+        for it in range(-1, slots + ACT_LAG + 1):
+            pieces = [(s, it - (first_slot[s] - INPUT_LEAD)) for s in range(1, NST)]
+            if 0 <= it - GAIN_LAG < slots:
+                to_features(units[(it - GAIN_LAG) // NJ], (it - GAIN_LAG) % NJ, 0)
+            run(to_rows, it - ACT_LAG)
+            for s, piece in pieces:
+                if 0 <= piece < 4:
+                    input_transposes(s, piece, tr_banks)
+            if 0 <= it - LATE_WEIGHTS < 4:
+                weight_words(2 + (it - LATE_WEIGHTS) // 2, (it - LATE_WEIGHTS) % 2, tr_banks)
+            if it == GAIN_TABLES:
+                tables.extend(gain_tables())
+            if 0 <= it - GAIN_LAG < slots:
+                to_features(units[(it - GAIN_LAG) // NJ], (it - GAIN_LAG) % NJ, 1)
+            run(products_to_normalise, it - NORM_LAG)
             if it >= 1:
-                run(a1_pe, it)
-            run(b_s, it - LB)
-            run(c_s, it - LC)
-            run(a2, it - LN)
-            for s in range(1, NST):
-                k = it - (first1[s] - LPREP[s])
-                if 0 <= k < 4:
-                    p_ev(s, k)
-                if k == 2:
-                    p_q(s, 0)
-                if k == 4:
-                    p_q(s, 1)
-            if it == 3:
-                w_q(2)
-            if it == 5:
-                w_q(3)
-            run(d_q, it - LD - DQ)
-            run(d_v, it - LD)
-            run(b_v, it - LB)
-            run(a1_v, it)
+                run(products_for_statistics, it)
+            run(first_gain, it - GAIN_LAG)
+            run(activate, it - ACT_LAG)
+            run(normalise_on_scalar, it - NORM_LAG)
+            for s, piece in pieces:
+                if 0 <= piece < 4:
+                    input_copy(s, piece)
+                if piece == 2:
+                    quantise_h(s)
+                if piece == 4:
+                    quantise_x(s)
+            if it - LATE_WEIGHTS in (2, 4):
+                quantise_weight(1 + (it - LATE_WEIGHTS) // 2)
+            run(quantise_hr, it - QUANT_LAG)
+            run(multiply, it - MUL_LAG)
+            run(finish_statistics, it - 1)
+            run(second_gain, it - GAIN_LAG)
+            run(normalise_on_vector, it - NORM_LAG)
+            run(statistics, it)
             for s in range(2, NST):
-                if it == max(first1[s] - LPREP[s] - LLOAD, -1):
-                    load(s)
+                if it == max(first_slot[s] - INPUT_LEAD - LOAD_LEAD, -1):
+                    load_rows(s)

from contextlib import ExitStack

import concourse.mybir as mybir
from concourse.masks import make_identity

F32 = mybir.dt.float32
BF16 = mybir.dt.bfloat16
U32 = mybir.dt.uint32
U8 = mybir.dt.uint8
FP8X4 = mybir.dt.float8_e4m3fn_x4
ACT = mybir.ActivationFunctionType
ALU = mybir.AluOpType

P = 128
ROWS = 4096
D = 512
ST = 512
NST = ROWS // ST
NJ = ST // P
NT = D // P
EPS = 1e-5
FLOPS = 4 * 2 * ROWS * D * D

CHAIN = 2
NORM_LAG = 4
GAIN_LAG = NORM_LAG + 5
ACT_LAG = GAIN_LAG + 4
MUL_LAG = ACT_LAG + 4
QUANT_LAG = MUL_LAG + 2
STAGE_GAP = 5
INPUT_LEAD = 5
LOAD_LEAD = 3
LATE_WEIGHTS = 10
GAIN_TABLES = 5
SCALAR_COPIES_UPTO = 2
VECTOR_NORMS_LAST_UNITS = 4
G_ROWS = 64


def unit_order():
    order = [(s, 1) for s in range(STAGE_GAP)]
    for s in range(NST - STAGE_GAP):
        order += [(s, 2), (s + STAGE_GAP, 1)]
    return order + [(s, 2) for s in range(NST - STAGE_GAP, NST)]


def tile_layernormgrucell_pa_t_kernel(tc, x, h, W_r, U_r, W_c, U_c, ln_gamma, ln_beta, out):
    nc = tc.nc
    x_v = x.rearrange("(s j p) k -> p s j k", s=NST, j=NJ)
    h_v = h.rearrange("(s j p) k -> p s j k", s=NST, j=NJ)
    out_v = out.rearrange("(s j p) f -> p s j f", s=NST, j=NJ)
    units = unit_order()
    slots = NJ * len(units)
    first_slot = {s: NJ * units.index((s, 1)) for s in range(NST)}

    with ExitStack() as ctx:
        ctx.enter_context(tc.manual_schedule())
        const = ctx.enter_context(tc.tile_pool(name="const", bufs=1))
        wpool = ctx.enter_context(tc.tile_pool(name="wpool", bufs=2))
        io = ctx.enter_context(tc.tile_pool(name="io", bufs=2))
        words = ctx.enter_context(tc.tile_pool(name="words", bufs=2))
        codes = ctx.enter_context(tc.tile_pool(name="codes", bufs=4))
        normed = ctx.enter_context(tc.tile_pool(name="normed", bufs=3))
        sums = ctx.enter_context(tc.tile_pool(name="sums", bufs=4))
        outs = ctx.enter_context(tc.tile_pool(name="outs", bufs=4))
        small = ctx.enter_context(tc.tile_pool(name="small", bufs=6))
        mx_banks = ctx.enter_context(tc.psum_pool(name="mx_banks", bufs=4))
        tr_banks = ctx.enter_context(tc.psum_pool(name="tr_banks", bufs=4))

        ident = const.tile([P, P], F32, name="ident")
        make_identity(nc, ident[:])
        minus_half = const.tile([P, 2 * CHAIN], F32, name="minus_half")
        nc.gpsimd.memset(minus_half[:], -0.5)
        warm = const.tile([P, 1], F32, name="warm")
        nc.vector.memset(warm[:], 0.0)
        nc.scalar.activation(out=warm[:], in_=warm[:], func=ACT.Sigmoid)

        def words_to_bank(pool, src, first):
            bank = pool.tile([P, 2, 2 * P], F32, tag="bank")
            for i in range(2):
                src32 = src[:, first + i, :].bitcast(F32)
                for u in range(2):
                    nc.tensor.transpose(bank[:, u, i * P:(i + 1) * P], src32[:, u * P:(u + 1) * P], ident[:])
            return bank

        def bank_to_words(dst, half, bank, on_scalar):
            dst32 = dst[:].bitcast(F32).rearrange("p (n u) -> p n u", u=2)[:, half * 2 * P:(half + 1) * 2 * P, :]
            if on_scalar:
                nc.scalar.copy(out=dst32, in_=bank[:].rearrange("p u n -> p n u"))
            else:
                nc.vector.tensor_copy(out=dst32, in_=bank[:].rearrange("p u n -> p n u"))

        def quantise(code_words, scales, src):
            nc.vector.quantize_mx(out=code_words.bitcast(FP8X4), scales=scales, in_=src)

        w_raw = {}
        w_words = {}
        w_codes = [const.tile([P, D], U32, name="w_codes%d" % i, align_bytes=64) for i in range(4)]
        w_scales = [const.tile([P, D], U8, name="w_scales%d" % i, align_bytes=64) for i in range(4)]

        def load_weight(i, w):
            raw = wpool.tile([P, NT, D], BF16, tag="raw", bufs=4)
            if i < 2:
                nc.sync.dma_start(out=raw[:].rearrange("p (u e) k -> p u e k", u=2),
                                  in_=w.rearrange("(u p e) k -> p u e k", u=2, e=2))
            else:
                nc.sync.dma_start(out=raw[:], in_=w.rearrange("(t p) k -> p t k", p=P))
            w_raw[i] = raw

        def weight_words(i, half, pool):
            if half == 0:
                grouped = wpool.tile([P, 4 * D], BF16, tag="grouped", align_bytes=64)
                w_words[i] = grouped
            bank_to_words(w_words[i], half, words_to_bank(pool, w_raw[i], 2 * half), half == 1)

        def quantise_weight(i):
            quantise(w_codes[i][:], w_scales[i][:], w_words[i][:])

        rows_in = {}
        h_words = {}
        x_words = {}
        in_banks = {}
        h_codes = {}
        x_codes = const.tile([P, NST, ST], U32, name="x_codes", align_bytes=64)
        x_scales = const.tile([P, NST, ST], U8, name="x_scales", align_bytes=64)

        def load_rows(s):
            h_sb = io.tile([P, NJ, D], BF16, tag="h_sb")
            nc.sync.dma_start(out=h_sb[:], in_=h_v[:, s])
            x_sb = io.tile([P, NJ, D], BF16, tag="x_sb")
            nc.sync.dma_start(out=x_sb[:], in_=x_v[:, s])
            rows_in[s] = (h_sb, x_sb)

        def input_transposes(s, piece, pool):
            if piece == 0:
                h_w = words.tile([P, 4 * ST], BF16, tag="h_w", bufs=6, align_bytes=64)
                x_w = words.tile([P, 4 * ST], BF16, tag="x_w", align_bytes=64)
                h_words[s] = h_w
                x_words[s] = x_w
            in_banks[(s, piece)] = words_to_bank(pool, rows_in[s][piece // 2], 2 * (piece % 2))

        def input_copy(s, piece):
            on_scalar = piece % 2 == 1 if s == 0 else s <= SCALAR_COPIES_UPTO
            bank_to_words(h_words[s] if piece < 2 else x_words[s], piece % 2, in_banks[(s, piece)], on_scalar)

        def quantise_h(s):
            c_w = codes.tile([P, ST], U32, tag="h_codes", align_bytes=64)
            c_s = codes.tile([P, ST], U8, tag="h_scales", align_bytes=64)
            quantise(c_w[:], c_s[:], h_words[s][:])
            h_codes[s] = (c_w, c_s)

        def quantise_x(s):
            quantise(x_codes[:, s, :], x_scales[:, s, :], x_words[s][:])

        def gain_tables():
            strided = params32[:].rearrange("p (u q e) -> p u e q", u=2, e=2)
            tables = []
            for stage in (1, 2):
                bank = tr_banks.tile([P, NT, P], F32, tag="bank")
                for t in range(NT):
                    chunk = strided[:, t // 2, t % 2, :] if stage == 1 else params32[:, t * P:(t + 1) * P]
                    nc.tensor.transpose(bank[:, t, :], chunk, ident[:])
                table = const.tile([P, 8, NT], F32, name="table%d" % stage)
                nc.vector.tensor_copy(out=table[:], in_=bank[:, :, 0:8].rearrange("p c i -> p i c"))
                bias = const.tile([P, NT], F32, name="bias%d" % stage)
                nc.vector.tensor_tensor(out=bias[:], in0=table[:, 2 + 2 * stage, :], in1=table[:, 3 + 2 * stage, :],
                                        op=ALU.add)
                tables.append((table, bias))
            return tables

        hr_codes = {}
        stat_banks = {}
        stat_parts = {}
        moments = {}

        def products(unit, j):
            s, stage = unit
            cols = slice(j * P, (j + 1) * P)
            a_w, a_s = h_codes[s] if stage == 1 else hr_codes[s]
            pair = []
            for lhs_w, lhs_s, i in ((a_w[:, cols], a_s[:, cols], 2 * stage - 2),
                                    (x_codes[:, s, cols], x_scales[:, s, cols], 2 * stage - 1)):
                bank = mx_banks.tile([P, D], F32, tag="bank")
                nc.tensor.matmul_mx(out=bank[:], lhsT=lhs_w.bitcast(FP8X4), lhsT_scale=lhs_s,
                                    rhs=w_codes[i][:].bitcast(FP8X4), rhs_scale=w_scales[i][:], start=True, stop=True)
                pair.append(bank)
            return pair

        def products_for_statistics(unit, j):
            stat_banks[(unit, j)] = products(unit, j)

        def statistics(unit, j):
            parts = small.tile([P, 2, 6], F32, tag="parts")
            for side in range(2):
                nc.vector.bn_stats(out=parts[:, side, :], in_=stat_banks[(unit, j)][side][:])
            stat_parts[(unit, j)] = parts

        def finish_statistics(unit, j):
            k = 2 * (j % CHAIN)
            if k == 0:
                mean_var = small.tile([P, 2 * CHAIN, 2], F32, tag="mean_var")
                moments[(unit, j // CHAIN)] = [mean_var]
            mean_var = moments[(unit, j // CHAIN)][0]
            for side in range(2):
                nc.vector.bn_aggr(out=mean_var[:, k + side, :], in_=stat_parts[(unit, j)][:, side, :])
            if j % CHAIN == CHAIN - 1:
                var_eps = small.tile([P, 2 * CHAIN], F32, tag="var_eps")
                nc.gpsimd.tensor_scalar(out=var_eps[:], in0=mean_var[:, :, 1], scalar1=1.0, scalar2=EPS,
                                        op0=ALU.mult, op1=ALU.add)
                rstd = small.tile([P, 2 * CHAIN], F32, tag="rstd")
                nc.gpsimd.tensor_tensor(out=rstd[:], in0=var_eps[:], in1=minus_half[:], op=ALU.pow)
                mean_rstd = small.tile([P, 2 * CHAIN], F32, tag="mean_rstd")
                nc.gpsimd.tensor_tensor(out=mean_rstd[:], in0=mean_var[:, :, 0], in1=rstd[:], op=ALU.mult)
                shift = small.tile([P, 2 * CHAIN], F32, tag="shift")
                nc.gpsimd.tensor_scalar(out=shift[:], in0=mean_rstd[:], scalar1=-1.0, scalar2=0.0,
                                        op0=ALU.mult, op1=ALU.add)
                moments[(unit, j // CHAIN)] += [rstd, shift]

        norm_banks = {}
        normal = {}

        def products_to_normalise(unit, j):
            norm_banks[(unit, j)] = products(unit, j)

        def on_vector(unit, j, side):
            return side == 1 and j % 2 == 1 and units.index(unit) >= len(units) - VECTOR_NORMS_LAST_UNITS

        def normalise(unit, j, vector_turn):
            if j == 0 and not vector_turn:
                n_a = normed.tile([P, NJ, D], F32, tag="n_a")
                n_b = normed.tile([P, NJ, D], F32, tag="n_b")
                normal[unit] = (n_a, n_b)
            mean_var, rstd, shift = moments[(unit, j // CHAIN)]
            for side in range(2):
                k = 2 * (j % CHAIN) + side
                if on_vector(unit, j, side) != vector_turn:
                    continue
                if vector_turn:
                    nc.vector.tensor_scalar(out=normal[unit][side][:, j, :], in0=norm_banks[(unit, j)][side][:],
                                            scalar1=mean_var[:, k, 0:1], scalar2=rstd[:, k:k + 1],
                                            op0=ALU.subtract, op1=ALU.mult)
                else:
                    nc.scalar.activation(out=normal[unit][side][:, j, :], in_=norm_banks[(unit, j)][side][:],
                                         func=ACT.Identity, bias=shift[:, k:k + 1], scale=rstd[:, k:k + 1])

        def normalise_on_scalar(unit, j):
            normalise(unit, j, False)

        def normalise_on_vector(unit, j):
            normalise(unit, j, True)

        feat_banks = {}
        summed = {}

        def to_features(unit, t, side):
            bank = tr_banks.tile([P, ST], F32, tag="bank")
            for j in range(NJ):
                nc.tensor.transpose(bank[:, j * P:(j + 1) * P], normal[unit][side][:, j, t * P:(t + 1) * P], ident[:])
            feat_banks[(unit, t, side)] = bank

        def first_gain(unit, t):
            if t == 0:
                z = sums.tile([P, NT, ST], F32, tag="z")
                summed[unit] = z
            table, bias = tables[unit[1] - 1]
            nc.scalar.activation(out=summed[unit][:, t, :], in_=feat_banks[(unit, t, 0)][:], func=ACT.Identity,
                                 bias=bias[:, t:t + 1], scale=table[:, 2 * unit[1] - 2, t:t + 1])

        def second_gain(unit, t):
            table, bias = tables[unit[1] - 1]
            z = summed[unit]
            nc.vector.scalar_tensor_tensor(out=z[:, t, :], in0=feat_banks[(unit, t, 1)][:],
                                           scalar=table[:, 2 * unit[1] - 1, t:t + 1], in1=z[:, t, :],
                                           op0=ALU.mult, op1=ALU.add)

        row_banks = {}

        def to_rows(unit, i):
            if unit[1] == 2:
                bank = tr_banks.tile([P, D], F32, tag="bank")
                for t in range(NT):
                    nc.tensor.transpose(bank[:, t * P:(t + 1) * P], summed[unit][:, t, i * P:(i + 1) * P], ident[:])
                row_banks[(unit, i)] = bank

        def activate(unit, i):
            if unit[1] == 1:
                nc.scalar.activation(out=summed[unit][:, i, :], in_=summed[unit][:, i, :], func=ACT.Sigmoid)
            else:
                c_sb = outs.tile([P, D], F32, tag="c_sb")
                nc.scalar.activation(out=c_sb[:], in_=row_banks[(unit, i)][:], func=ACT.Tanh)
                nc.sync.dma_start(out=out_v[:, unit[0], i, :], in_=c_sb[:])

        hr_words = {}

        def multiply(unit, i):
            s, stage = unit
            if stage == 2:
                return
            if i == 0:
                hr_w = words.tile([P, 4 * ST], BF16, tag="hr_w", align_bytes=64)
                hr_words[s] = hr_w
            for engine, lo, hi in ((nc.gpsimd, 0, G_ROWS), (nc.vector, G_ROWS, P)):
                rows = slice(i * P + lo, i * P + hi)
                engine.tensor_tensor(out=hr_words[s][:].rearrange("p (r t) -> p r t", t=4)[:, rows, :],
                                     in0=summed[unit][:, :, rows].rearrange("p t r -> p r t"),
                                     in1=h_words[s][:].rearrange("p (r t) -> p r t", t=4)[:, rows, :], op=ALU.mult)

        def quantise_hr(unit, i):
            s, stage = unit
            if stage == 2:
                return
            if i == 0:
                c_w = codes.tile([P, ST], U32, tag="hr_codes", bufs=5, align_bytes=64)
                c_s = codes.tile([P, ST], U8, tag="hr_scales", bufs=5, align_bytes=64)
                hr_codes[s] = (c_w, c_s)
            c_w, c_s = hr_codes[s]
            quantise(c_w[:, i * P:(i + 1) * P], c_s[:, i * P:(i + 1) * P], hr_words[s][:, i * 4 * P:(i + 1) * 4 * P])

        def run(step, slot):
            if 0 <= slot < slots:
                step(units[slot // NJ], slot % NJ)

        load_weight(0, W_r)
        load_rows(0)
        load_weight(1, U_r)
        params = const.tile([P, D], BF16, name="params")
        nc.vector.memset(params[:], 0.0)
        nc.sync.dma_start(out=params[0:4, :], in_=ln_gamma)
        nc.sync.dma_start(out=params[4:8, :], in_=ln_beta)
        load_rows(1)
        load_weight(2, W_c)
        load_weight(3, U_c)

        weight_words(0, 0, mx_banks)
        weight_words(0, 1, mx_banks)
        for piece in range(4):
            input_transposes(0, piece, mx_banks if piece < 2 else tr_banks)
            input_copy(0, piece)
            if piece == 1:
                quantise_weight(0)
        quantise_h(0)
        weight_words(1, 0, tr_banks)
        weight_words(1, 1, tr_banks)
        quantise_x(0)
        quantise_weight(1)
        params32 = const.tile([P, D], F32, name="params32")
        nc.gpsimd.tensor_scalar(out=params32[:], in0=params[:], scalar1=1.0, scalar2=0.0, op0=ALU.mult, op1=ALU.add)
        run(products_for_statistics, 0)

        tables = []
        for it in range(-1, slots + ACT_LAG + 1):
            pieces = [(s, it - (first_slot[s] - INPUT_LEAD)) for s in range(1, NST)]
            if 0 <= it - GAIN_LAG < slots:
                to_features(units[(it - GAIN_LAG) // NJ], (it - GAIN_LAG) % NJ, 0)
            run(to_rows, it - ACT_LAG)
            for s, piece in pieces:
                if 0 <= piece < 4:
                    input_transposes(s, piece, tr_banks)
            if 0 <= it - LATE_WEIGHTS < 4:
                weight_words(2 + (it - LATE_WEIGHTS) // 2, (it - LATE_WEIGHTS) % 2, tr_banks)
            if it == GAIN_TABLES:
                tables.extend(gain_tables())
            if 0 <= it - GAIN_LAG < slots:
                to_features(units[(it - GAIN_LAG) // NJ], (it - GAIN_LAG) % NJ, 1)
            run(products_to_normalise, it - NORM_LAG)
            if it >= 1:
                run(products_for_statistics, it)
            run(first_gain, it - GAIN_LAG)
            run(activate, it - ACT_LAG)
            run(normalise_on_scalar, it - NORM_LAG)
            for s, piece in pieces:
                if 0 <= piece < 4:
                    input_copy(s, piece)
                if piece == 2:
                    quantise_h(s)
                if piece == 4:
                    quantise_x(s)
            if it - LATE_WEIGHTS in (2, 4):
                quantise_weight(1 + (it - LATE_WEIGHTS) // 2)
            run(quantise_hr, it - QUANT_LAG)
            run(multiply, it - MUL_LAG)
            run(finish_statistics, it - 1)
            run(second_gain, it - GAIN_LAG)
            run(normalise_on_vector, it - NORM_LAG)
            run(statistics, it)
            for s in range(2, NST):
                if it == max(first_slot[s] - INPUT_LEAD - LOAD_LEAD, -1):
                    load_rows(s)
